import numpy as np
import ml_dtypes


def mxq(x, axis, fmt="e4m3"):
    dtype, down = {"e4m3": (ml_dtypes.float8_e4m3fn, 7), "e5m2": (ml_dtypes.float8_e5m2, 14)}[fmt]
    v = np.moveaxis(np.asarray(x, np.float32).astype(ml_dtypes.bfloat16).astype(np.float64), axis, -1)
    blocks = v.reshape(v.shape[:-1] + (-1, 32))
    amax = np.abs(blocks).max(-1, keepdims=True)
    byte = np.maximum(np.where(amax > 0, np.frexp(amax)[1] - 1 + 127, 0) - down, 1)
    scale = np.exp2(byte - 127.0)
    codes = (blocks / scale).astype(np.float32).astype(dtype).astype(np.float64)
    return np.moveaxis((codes * scale).reshape(v.shape), -1, axis)


WIDE = False


def mx_kscale(k):
    if not WIDE:
        return np.ones(k)
    levels = np.array([10, -10, 5, -5, 0])
    a = np.random.permutation(np.resize(levels, k // 512 * 4)).reshape(k // 512, 4)
    idx = np.arange(k)
    return np.exp2(a[idx // 512, idx % 128 // 32])


BF16 = ml_dtypes.bfloat16


def bf(x):
    return np.asarray(x, np.float32).astype(BF16)


def f64(x):
    return np.asarray(x).astype(np.float64)


E2M1 = np.array([0.0, 0.5, 1.0, 1.5, 2.0, 3.0, 4.0, 6.0, -0.0, -0.5, -1.0, -1.5, -2.0, -3.0, -4.0, -6.0])


def pack_weight(w, fmt):
    k, n = w.shape
    w = f64(bf(w)).reshape(k // 32, 32, n)
    amax = np.abs(w).max(1)
    if fmt == "e4m3":
        byte = np.frexp(amax)[1] - 1 + 127 - 7
    else:
        mant, ex = np.frexp(amax / 6.0)
        byte = np.where(mant > 0.5, ex, ex - 1) + 127
    byte = np.clip(np.where(amax > 0, byte, 1), 1, 254)
    scaled = (w * np.exp2(127.0 - byte)[:, None, :]).reshape(k, n).astype(np.float32)
    by_word = np.ascontiguousarray(scaled.reshape(k // 512, 128, 4, n).transpose(0, 1, 3, 2))
    if fmt == "e4m3":
        words = by_word.astype(ml_dtypes.float8_e4m3fn).view(np.uint8)
    else:
        c = by_word.astype(ml_dtypes.float4_e2m1fn).view(np.uint8) & 0xF
        words = c[..., 0::2] | (c[..., 1::2] << 4)
    return np.ascontiguousarray(words), np.ascontiguousarray(byte.astype(np.uint8).reshape(k // 512, 16, n))


def unpack_weight(words, scales, fmt):
    g, p, n, _ = words.shape
    if fmt == "e4m3":
        vals = np.ascontiguousarray(words).view(ml_dtypes.float8_e4m3fn).astype(np.float64)
    else:
        nib = np.empty((g, p, n, 4), np.uint8)
        nib[..., 0::2] = words & 0xF
        nib[..., 1::2] = words >> 4
        vals = E2M1[nib]
    vals = vals * np.repeat(np.exp2(scales.astype(np.float64) - 127.0), 8, axis=1)[..., None]
    return vals.transpose(0, 1, 3, 2).reshape(g * 512, n)


N, T, D, B0, C, P0, V1, P1, V2 = 8, 1024, 512, 254, 2, 512, 256, 512, 1024
MU = 0.25
SIG = 2.0
FMT = "e4m3"


def softmax(v):
    e = np.exp(v - v.max(-1, keepdims=True))
    return e / e.sum(-1, keepdims=True)


def setup_inputs():
    s, t = mx_kscale(D), mx_kscale(P0)
    hw = np.random.standard_normal((D, B0 + C)) * SIG / np.sqrt(D)
    hw[:, B0:] = hw[:, B0:] / SIG + (np.log(B0) + 0.5 * SIG * SIG) / (MU * D)
    x = bf((np.random.standard_normal((N, T, D)) + MU) * s)
    head_words, head_scales = pack_weight(hw / s[:, None], FMT)
    proj_words, proj_scales = pack_weight(np.random.standard_normal((D, P0)) / np.sqrt(D) / s[:, None] * t, FMT)
    tail_words, tail_scales = pack_weight(np.random.standard_normal((P0, V1)) * SIG / np.sqrt(P0) / t[:, None], FMT)
    return {"x": x,
            "head_weight_words": head_words, "head_weight_scales": head_scales,
            "tail_proj_0_words": proj_words, "tail_proj_0_scales": proj_scales,
            "tail_w_0_words": tail_words, "tail_w_0_scales": tail_scales}


def reference(x, head_weight_words, head_weight_scales, tail_proj_0_words, tail_proj_0_scales, tail_w_0_words, tail_w_0_scales):
    xq = mxq(f64(x), 2, "e4m3")
    head_sm = softmax(xq @ unpack_weight(head_weight_words, head_weight_scales, FMT))
    h = xq @ unpack_weight(tail_proj_0_words, tail_proj_0_scales, FMT)
    tail_sm = softmax(mxq(h, 2, "e4m3") @ unpack_weight(tail_w_0_words, tail_w_0_scales, FMT))
    probs = np.concatenate([head_sm[..., :B0], tail_sm * head_sm[..., B0:B0 + 1]], axis=-1)
    return probs, head_sm[..., B0 + 1:B0 + C]

@@ -1,0 +1,302 @@
+from contextlib import ExitStack
+
+import concourse.mybir as mybir
+from concourse.masks import make_identity
+
+F32 = mybir.dt.float32
+BF16 = mybir.dt.bfloat16
+I32 = mybir.dt.int32
+U32 = mybir.dt.uint32
+U8 = mybir.dt.uint8
+FP8X4 = mybir.dt.float8_e4m3fn_x4
+ALU = mybir.AluOpType
+ACT = mybir.ActivationFunctionType
+
+P = 128
+PACK = 4
+TOKENS = 8 * 1024
+FEATURES = 512
+HEAD = 256
+HEAD_TOKENS = 254
+PROJ = 512
+TAIL = 256
+PROBS = HEAD_TOKENS + TAIL
+PER_PARTITION = TOKENS // P
+BLOCK = 4
+N_BLOCKS = PER_PARTITION // BLOCK
+PAIR = 2
+N_PAIRS = PER_PARTITION // PAIR
+
+PROJ_AT = 0
+HEAD_AT = PROJ
+TAIL_AT = PROJ + HEAD
+ALL_COLS = PROJ + HEAD + TAIL
+
+FLOPS = 2 * TOKENS * FEATURES * ALL_COLS
+
+
+def tile_adaptiveinputsoftmax_pa_t_kernel(
+    tc,
+    x,
+    head_weight_words,
+    head_weight_scales,
+    tail_proj_0_words,
+    tail_proj_0_scales,
+    tail_w_0_words,
+    tail_w_0_scales,
+    out_0,
+    out_1,
+):
+    nc = tc.nc
+    x_blocks = x.flatten_outer_dims().rearrange(
+        "(p s j) d -> s p (j d)", p=P, s=N_BLOCKS, j=BLOCK
+    )
+    probs_blocks = out_0.flatten_outer_dims().rearrange(
+        "(p s j) d -> s p (j d)", p=P, s=N_BLOCKS, j=BLOCK
+    )
+    other_cluster = out_1.rearrange("n t o -> (n t o)").rearrange("(p c) -> p c", p=P)
+
+    with ExitStack() as ctx:
+        const = ctx.enter_context(tc.tile_pool(name="const", bufs=1))
+        x_pool = ctx.enter_context(tc.tile_pool(name="x_pool", bufs=N_BLOCKS))
+        grouped = ctx.enter_context(tc.tile_pool(name="grouped", bufs=2))
+        x_mx = ctx.enter_context(tc.tile_pool(name="x_mx", bufs=5))
+        h_rows = ctx.enter_context(tc.tile_pool(name="h_rows", bufs=2 * PAIR))
+        h_mx = ctx.enter_context(tc.tile_pool(name="h_mx", bufs=3))
+        soft = ctx.enter_context(tc.tile_pool(name="soft", bufs=3))
+        result = ctx.enter_context(tc.tile_pool(name="result", bufs=3))
+        bank_xt = ctx.enter_context(tc.psum_pool(name="bank_xt", bufs=1))
+        bank_ht = ctx.enter_context(tc.psum_pool(name="bank_ht", bufs=1))
+        bank_h = ctx.enter_context(tc.psum_pool(name="bank_h", bufs=PAIR))
+        bank_logits = ctx.enter_context(tc.psum_pool(name="bank_logits", bufs=2 * PAIR))
+        ctx.enter_context(tc.manual_schedule())
+
+        w_scales = const.tile([P, ALL_COLS], U8, align_bytes=64)
+        nc.vector.memset(w_scales[:].bitcast(I32), 0)
+        w_words = const.tile([P, ALL_COLS], U32, align_bytes=64)
+
+        warm_in = const.tile([P, 1], F32)
+        warm_out = const.tile([P, 1], F32)
+        nc.vector.memset(warm_in[:], 0.0)
+        nc.scalar.activation(out=warm_out[:], in_=warm_in[:], func=ACT.Exp)
+
+        ident_f32 = const.tile([P, P], F32)
+        make_identity(nc, ident_f32[:])
+        ident_bf16 = const.tile([P, P], BF16)
+        make_identity(nc, ident_bf16[:])
+
+        clusters = const.tile([P, PER_PARTITION, 2], F32)
+
+        x_sb = {}
+
+        def load_x(s):
+            x_block = x_pool.tile([P, BLOCK, FEATURES], BF16)
+            nc.sync.dma_start(
+                out=x_block[:].rearrange("p j d -> p (j d)"), in_=x_blocks[s]
+            )
+            x_sb[s] = x_block
+
+        def load_weight(words, scales, at, cols):
+            for quadrant in range(4):
+                nc.sync.dma_start(
+                    out=w_scales[32 * quadrant : 32 * quadrant + 4, at : at + cols].bitcast(I32),
+                    in_=scales[0, 4 * quadrant : 4 * quadrant + 4, :].bitcast(I32),
+                )
+            nc.sync.dma_start(
+                out=w_words[:, at : at + cols].bitcast(I32),
+                in_=words[0].rearrange("p n t -> p (n t)").bitcast(I32),
+            )
+
+        load_x(0)
+        load_weight(tail_proj_0_words, tail_proj_0_scales, PROJ_AT, PROJ)
+        load_x(1)
+        load_weight(head_weight_words, head_weight_scales, HEAD_AT, HEAD)
+        load_weight(tail_w_0_words, tail_w_0_scales, TAIL_AT, TAIL)
+        for s in range(2, N_BLOCKS):
+            load_x(s)
+
+        xt_bank, x_grouped, x_codes, x_scales = {}, {}, {}, {}
+        h_bank, h_sb, ht_bank, h_grouped, h_codes, h_scales = {}, {}, {}, {}, {}, {}
+        logit_bank, neg_max, exps, sums, probs = {}, {}, {}, {}, {}
+
+        def transpose_x(i):
+            xt = bank_xt.tile([P, PAIR, 2, P], F32)
+            for jj in range(PAIR):
+                c = PAIR * i + jj
+                words = x_sb[c // BLOCK][:, c % BLOCK, :].bitcast(F32)
+                for u in range(2):
+                    nc.tensor.transpose(
+                        out=xt[:, jj, u, :],
+                        in_=words[:, u : FEATURES // 2 : 2],
+                        identity=ident_f32[:],
+                    )
+            xt_bank[i] = xt
+
+        def group_x(i):
+            xg = grouped.tile([P, PAIR, P, PACK], BF16, align_bytes=64)
+            nc.vector.tensor_copy(
+                out=xg[:].bitcast(F32), in_=xt_bank[i][:].rearrange("p j u r -> p j r u")
+            )
+            x_grouped[i] = xg
+
+        def quantise(pool, values):
+            codes = pool.tile([P, PAIR * P], U32, align_bytes=64)
+            scales = pool.tile([P, PAIR * P], U8, align_bytes=64)
+            nc.vector.quantize_mx(
+                out=codes[:].bitcast(FP8X4),
+                scales=scales[:],
+                in_=values[:].rearrange("p j r t -> p (j r t)"),
+            )
+            return codes, scales
+
+        def multiply(out, codes, scales, jj, at, cols):
+            nc.tensor.matmul_mx(
+                out=out,
+                lhsT=codes[:, jj * P : (jj + 1) * P].bitcast(FP8X4),
+                lhsT_scale=scales[:, jj * P : (jj + 1) * P],
+                rhs=w_words[:, at : at + cols].bitcast(FP8X4),
+                rhs_scale=w_scales[:, at : at + cols],
+                start=True,
+                stop=True,
+            )
+
+        def project(i):
+            for jj in range(PAIR):
+                h_acc = bank_h.tile([P, PROJ], F32)
+                multiply(h_acc[:], x_codes[i], x_scales[i], jj, PROJ_AT, PROJ)
+                h_bank[i, jj] = h_acc
+
+        def round_h(i):
+            for jj in range(PAIR):
+                h_tile = h_rows.tile([P, PACK, P], BF16)
+                by_slot = h_bank[i, jj][:].rearrange("r (p t) -> r t p", t=PACK)
+                if jj == 0:
+                    nc.vector.tensor_copy(out=h_tile[:], in_=by_slot)
+                else:
+                    nc.scalar.copy(out=h_tile[:], in_=by_slot)
+                h_sb[i, jj] = h_tile
+
+        def transpose_h(i):
+            ht = bank_ht.tile([P, PAIR, PACK, P], BF16)
+            for jj in range(PAIR):
+                for t in range(PACK):
+                    nc.tensor.transpose(
+                        out=ht[:, jj, t, :], in_=h_sb[i, jj][:, t, :], identity=ident_bf16[:]
+                    )
+            ht_bank[i] = ht
+
+        def group_h(i):
+            hg = grouped.tile([P, PAIR, P, PACK], BF16, align_bytes=64)
+            nc.scalar.copy(out=hg[:], in_=ht_bank[i][:].rearrange("p j t r -> p j r t"))
+            h_grouped[i] = hg
+
+        def logits(i):
+            for jj in range(PAIR):
+                both = bank_logits.tile([P, 2, HEAD], F32)
+                multiply(both[:, 0, :], x_codes[i], x_scales[i], jj, HEAD_AT, HEAD)
+                multiply(both[:, 1, :], h_codes[i], h_scales[i], jj, TAIL_AT, TAIL)
+                logit_bank[i, jj] = both
+
+        def row_max(i):
+            minus_max = soft.tile([P, PAIR, 2], F32)
+            for jj in range(PAIR):
+                nc.vector.tensor_reduce(
+                    out=minus_max[:, jj, :],
+                    in_=logit_bank[i, jj][:],
+                    axis=mybir.AxisListType.X,
+                    op=ALU.max,
+                    negate=True,
+                )
+            neg_max[i] = minus_max
+
+        def exponentials(i):
+            e = soft.tile([P, PAIR, 2, HEAD], F32)
+            e_sum = soft.tile([P, PAIR, 2], F32)
+            for jj in range(PAIR):
+                for half in range(2):
+                    nc.scalar.activation(
+                        out=e[:, jj, half, :],
+                        in_=logit_bank[i, jj][:, half, :],
+                        func=ACT.Exp,
+                        bias=neg_max[i][:, jj, half : half + 1],
+                        accum_out=e_sum[:, jj, half : half + 1],
+                    )
+            exps[i] = e
+            sums[i] = e_sum
+
+        def normalise(i):
+            e = exps[i]
+            if i % 2 == 0:
+                probs_block = result.tile([P, BLOCK, PROBS], F32)
+                probs[i // 2] = probs_block
+            out_rows = probs[i // 2]
+            inv_sum = soft.tile([P, PAIR, 2], F32)
+            nc.vector.reciprocal(out=inv_sum[:], in_=sums[i][:])
+            pair_clusters = clusters[:, PAIR * i : PAIR * (i + 1), :]
+            nc.gpsimd.tensor_tensor(
+                out=pair_clusters,
+                in0=e[:, :, 0, HEAD_TOKENS:HEAD],
+                in1=inv_sum[:, :, 0:1].to_broadcast([P, PAIR, 2]),
+                op=ALU.mult,
+            )
+            tail_factor = soft.tile([P, PAIR, 1], F32)
+            nc.gpsimd.tensor_tensor(
+                out=tail_factor[:],
+                in0=inv_sum[:, :, 1:2],
+                in1=pair_clusters[:, :, 0:1],
+                op=ALU.mult,
+            )
+            for jj in range(PAIR):
+                j = PAIR * (i % 2) + jj
+                nc.gpsimd.tensor_scalar(
+                    out=out_rows[:, j, 0:HEAD_TOKENS],
+                    in0=e[:, jj, 0, 0:HEAD_TOKENS],
+                    scalar1=inv_sum[:, jj, 0:1],
+                    scalar2=0.0,
+                    op0=ALU.mult,
+                    op1=ALU.add,
+                )
+                nc.gpsimd.tensor_scalar(
+                    out=out_rows[:, j, HEAD_TOKENS:PROBS],
+                    in0=e[:, jj, 1, :],
+                    scalar1=tail_factor[:, jj, :],
+                    scalar2=0.0,
+                    op0=ALU.mult,
+                    op1=ALU.add,
+                )
+            if i % 2 == 1:
+                nc.sync.dma_start(
+                    out=probs_blocks[i // 2], in_=out_rows[:].rearrange("p j d -> p (j d)")
+                )
+
+        def live(i):
+            return 0 <= i < N_PAIRS
+
+        for r in range(-3, N_PAIRS + 1):
+            if live(r + 3):
+                transpose_x(r + 3)
+            if live(r + 1):
+                transpose_h(r + 1)
+            if live(r + 2):
+                project(r + 2)
+            if live(r):
+                logits(r)
+            if live(r + 3):
+                group_x(r + 3)
+            if live(r + 1):
+                group_h(r + 1)
+            if live(r + 2):
+                round_h(r + 2)
+            if live(r - 1):
+                normalise(r - 1)
+            if live(r + 3):
+                x_codes[r + 3], x_scales[r + 3] = quantise(x_mx, x_grouped[r + 3])
+            if live(r):
+                row_max(r)
+                exponentials(r)
+            if live(r + 1):
+                h_codes[r + 1], h_scales[r + 1] = quantise(h_mx, h_grouped[r + 1])
+
+        other = const.tile([P, PER_PARTITION], F32)
+        nc.vector.tensor_copy(out=other[:], in_=clusters[:, :, 1])
+        nc.sync.dma_start(out=other_cluster, in_=other[:])

@@ -60,10 +60,10 @@ def tile_adaptiveinputsoftmax_pa_t_kernel(
         const = ctx.enter_context(tc.tile_pool(name="const", bufs=1))
         x_pool = ctx.enter_context(tc.tile_pool(name="x_pool", bufs=N_BLOCKS))
         grouped = ctx.enter_context(tc.tile_pool(name="grouped", bufs=2))
-        x_mx = ctx.enter_context(tc.tile_pool(name="x_mx", bufs=5))
-        h_rows = ctx.enter_context(tc.tile_pool(name="h_rows", bufs=2 * PAIR))
+        x_mx = ctx.enter_context(tc.tile_pool(name="x_mx", bufs=6))
+        h_rows = ctx.enter_context(tc.tile_pool(name="h_rows", bufs=3 * PAIR))
         h_mx = ctx.enter_context(tc.tile_pool(name="h_mx", bufs=3))
-        soft = ctx.enter_context(tc.tile_pool(name="soft", bufs=3))
+        soft = ctx.enter_context(tc.tile_pool(name="soft", bufs=4))
         result = ctx.enter_context(tc.tile_pool(name="result", bufs=3))
         bank_xt = ctx.enter_context(tc.psum_pool(name="bank_xt", bufs=1))
         bank_ht = ctx.enter_context(tc.psum_pool(name="bank_ht", bufs=1))
@@ -166,15 +166,14 @@ def tile_adaptiveinputsoftmax_pa_t_kernel(
                 multiply(h_acc[:], x_codes[i], x_scales[i], jj, PROJ_AT, PROJ)
                 h_bank[i, jj] = h_acc
 
-        def round_h(i):
-            for jj in range(PAIR):
-                h_tile = h_rows.tile([P, PACK, P], BF16)
-                by_slot = h_bank[i, jj][:].rearrange("r (p t) -> r t p", t=PACK)
-                if jj == 0:
-                    nc.vector.tensor_copy(out=h_tile[:], in_=by_slot)
-                else:
-                    nc.scalar.copy(out=h_tile[:], in_=by_slot)
-                h_sb[i, jj] = h_tile
+        def round_h(i, jj):
+            h_tile = h_rows.tile([P, PACK, P], BF16)
+            by_slot = h_bank[i, jj][:].rearrange("r (p t) -> r t p", t=PACK)
+            if jj == 0:
+                nc.vector.tensor_copy(out=h_tile[:], in_=by_slot)
+            else:
+                nc.scalar.copy(out=h_tile[:], in_=by_slot)
+            h_sb[i, jj] = h_tile
 
         def transpose_h(i):
             ht = bank_ht.tile([P, PAIR, PACK, P], BF16)
@@ -209,20 +208,20 @@ def tile_adaptiveinputsoftmax_pa_t_kernel(
                 )
             neg_max[i] = minus_max
 
-        def exponentials(i):
-            e = soft.tile([P, PAIR, 2, HEAD], F32)
-            e_sum = soft.tile([P, PAIR, 2], F32)
-            for jj in range(PAIR):
-                for half in range(2):
-                    nc.scalar.activation(
-                        out=e[:, jj, half, :],
-                        in_=logit_bank[i, jj][:, half, :],
-                        func=ACT.Exp,
-                        bias=neg_max[i][:, jj, half : half + 1],
-                        accum_out=e_sum[:, jj, half : half + 1],
-                    )
-            exps[i] = e
-            sums[i] = e_sum
+        def exponentials(i, jj):
+            if jj == 0:
+                e = soft.tile([P, PAIR, 2, HEAD], F32)
+                e_sum = soft.tile([P, PAIR, 2], F32)
+                exps[i] = e
+                sums[i] = e_sum
+            for half in range(2):
+                nc.scalar.activation(
+                    out=exps[i][:, jj, half, :],
+                    in_=logit_bank[i, jj][:, half, :],
+                    func=ACT.Exp,
+                    bias=neg_max[i][:, jj, half : half + 1],
+                    accum_out=sums[i][:, jj, half : half + 1],
+                )
 
         def normalise(i):
             e = exps[i]
@@ -239,13 +238,6 @@ def tile_adaptiveinputsoftmax_pa_t_kernel(
                 in1=inv_sum[:, :, 0:1].to_broadcast([P, PAIR, 2]),
                 op=ALU.mult,
             )
-            tail_factor = soft.tile([P, PAIR, 1], F32)
-            nc.gpsimd.tensor_tensor(
-                out=tail_factor[:],
-                in0=inv_sum[:, :, 1:2],
-                in1=pair_clusters[:, :, 0:1],
-                op=ALU.mult,
-            )
             for jj in range(PAIR):
                 j = PAIR * (i % 2) + jj
                 nc.gpsimd.tensor_scalar(
@@ -259,10 +251,10 @@ def tile_adaptiveinputsoftmax_pa_t_kernel(
                 nc.gpsimd.tensor_scalar(
                     out=out_rows[:, j, HEAD_TOKENS:PROBS],
                     in0=e[:, jj, 1, :],
-                    scalar1=tail_factor[:, jj, :],
-                    scalar2=0.0,
+                    scalar1=inv_sum[:, jj, 1:2],
+                    scalar2=pair_clusters[:, jj, 0:1],
                     op0=ALU.mult,
-                    op1=ALU.add,
+                    op1=ALU.mult,
                 )
             if i % 2 == 1:
                 nc.sync.dma_start(
@@ -272,28 +264,32 @@ def tile_adaptiveinputsoftmax_pa_t_kernel(
         def live(i):
             return 0 <= i < N_PAIRS
 
-        for r in range(-3, N_PAIRS + 1):
-            if live(r + 3):
-                transpose_x(r + 3)
+        for r in range(-4, N_PAIRS + 2):
+            if live(r + 4):
+                transpose_x(r + 4)
             if live(r + 1):
                 transpose_h(r + 1)
-            if live(r + 2):
-                project(r + 2)
+            if live(r + 3):
+                project(r + 3)
             if live(r):
                 logits(r)
-            if live(r + 3):
-                group_x(r + 3)
+            if live(r - 2):
+                normalise(r - 2)
+            if live(r + 4):
+                group_x(r + 4)
+            if live(r - 1):
+                exponentials(r - 1, 0)
             if live(r + 1):
                 group_h(r + 1)
-            if live(r + 2):
-                round_h(r + 2)
             if live(r - 1):
-                normalise(r - 1)
+                exponentials(r - 1, 1)
             if live(r + 3):
-                x_codes[r + 3], x_scales[r + 3] = quantise(x_mx, x_grouped[r + 3])
+                round_h(r + 3, 0)
+                round_h(r + 3, 1)
+            if live(r + 4):
+                x_codes[r + 4], x_scales[r + 4] = quantise(x_mx, x_grouped[r + 4])
             if live(r):
                 row_max(r)
-                exponentials(r)
             if live(r + 1):
                 h_codes[r + 1], h_scales[r + 1] = quantise(h_mx, h_grouped[r + 1])
 

@@ -24,8 +24,15 @@ PROBS = HEAD_TOKENS + TAIL
 PER_PARTITION = TOKENS // P
 BLOCK = 4
 N_BLOCKS = PER_PARTITION // BLOCK
+STORE_CUT = (BLOCK - 1) * PROBS + HEAD_TOKENS
+assert (4 * STORE_CUT) % 32 == 0 and (4 * BLOCK * PROBS) % 32 == 0
 PAIR = 2
 N_PAIRS = PER_PARTITION // PAIR
+PAIR_WORDS = PAIR * P
+
+X_AHEAD = 5
+PROJ_AHEAD = 3
+H_AHEAD = 1
 
 PROJ_AT = 0
 HEAD_AT = PROJ
@@ -59,16 +66,15 @@ def tile_adaptiveinputsoftmax_pa_t_kernel(
     with ExitStack() as ctx:
         const = ctx.enter_context(tc.tile_pool(name="const", bufs=1))
         x_pool = ctx.enter_context(tc.tile_pool(name="x_pool", bufs=N_BLOCKS))
-        grouped = ctx.enter_context(tc.tile_pool(name="grouped", bufs=2))
-        x_mx = ctx.enter_context(tc.tile_pool(name="x_mx", bufs=6))
+        grouped = ctx.enter_context(tc.tile_pool(name="grouped", bufs=3))
+        packed = ctx.enter_context(tc.tile_pool(name="packed", bufs=X_AHEAD + 2))
         h_rows = ctx.enter_context(tc.tile_pool(name="h_rows", bufs=3 * PAIR))
-        h_mx = ctx.enter_context(tc.tile_pool(name="h_mx", bufs=3))
         soft = ctx.enter_context(tc.tile_pool(name="soft", bufs=4))
         result = ctx.enter_context(tc.tile_pool(name="result", bufs=3))
-        bank_xt = ctx.enter_context(tc.psum_pool(name="bank_xt", bufs=1))
+        bank_xt = ctx.enter_context(tc.psum_pool(name="bank_xt", bufs=2))
         bank_ht = ctx.enter_context(tc.psum_pool(name="bank_ht", bufs=1))
         bank_h = ctx.enter_context(tc.psum_pool(name="bank_h", bufs=PAIR))
-        bank_logits = ctx.enter_context(tc.psum_pool(name="bank_logits", bufs=2 * PAIR))
+        bank_logits = ctx.enter_context(tc.psum_pool(name="bank_logits", bufs=3))
         ctx.enter_context(tc.manual_schedule())
 
         w_scales = const.tile([P, ALL_COLS], U8, align_bytes=64)
@@ -115,9 +121,22 @@ def tile_adaptiveinputsoftmax_pa_t_kernel(
         for s in range(2, N_BLOCKS):
             load_x(s)
 
-        xt_bank, x_grouped, x_codes, x_scales = {}, {}, {}, {}
-        h_bank, h_sb, ht_bank, h_grouped, h_codes, h_scales = {}, {}, {}, {}, {}, {}
-        logit_bank, neg_max, exps, sums, probs = {}, {}, {}, {}, {}
+        xt_bank, h_bank, h_sb, ht_bank, logit_bank = {}, {}, {}, {}, {}
+        to_quantise, codes, scales = {}, {}, {}
+        neg_max, exps, sums, probs = {}, {}, {}, {}
+
+        def live(i):
+            return 0 <= i < N_PAIRS
+
+        def open_round(r):
+            values = grouped.tile([P, 2 * PAIR_WORDS * PACK], BF16, align_bytes=64)
+            to_quantise[r] = values
+
+        def values_of_x(i):
+            return to_quantise[i - X_AHEAD][:, 0 : PAIR_WORDS * PACK]
+
+        def values_of_h(i):
+            return to_quantise[i - H_AHEAD][:, PAIR_WORDS * PACK : 2 * PAIR_WORDS * PACK]
 
         def transpose_x(i):
             xt = bank_xt.tile([P, PAIR, 2, P], F32)
@@ -133,42 +152,50 @@ def tile_adaptiveinputsoftmax_pa_t_kernel(
             xt_bank[i] = xt
 
         def group_x(i):
-            xg = grouped.tile([P, PAIR, P, PACK], BF16, align_bytes=64)
             nc.vector.tensor_copy(
-                out=xg[:].bitcast(F32), in_=xt_bank[i][:].rearrange("p j u r -> p j r u")
+                out=values_of_x(i).bitcast(F32).rearrange("p (j r u) -> p j r u", j=PAIR, u=2),
+                in_=xt_bank[i][:].rearrange("p j u r -> p j r u"),
             )
-            x_grouped[i] = xg
 
-        def quantise(pool, values):
-            codes = pool.tile([P, PAIR * P], U32, align_bytes=64)
-            scales = pool.tile([P, PAIR * P], U8, align_bytes=64)
+        def quantise(r):
+            round_codes = packed.tile([P, 2 * PAIR_WORDS], U32, align_bytes=64)
+            round_scales = packed.tile([P, 2 * PAIR_WORDS], U8, align_bytes=64)
+            first = 0 if live(r + X_AHEAD) else PAIR_WORDS
+            end = 2 * PAIR_WORDS if live(r + H_AHEAD) else PAIR_WORDS
             nc.vector.quantize_mx(
-                out=codes[:].bitcast(FP8X4),
-                scales=scales[:],
-                in_=values[:].rearrange("p j r t -> p (j r t)"),
+                out=round_codes[:, first:end].bitcast(FP8X4),
+                scales=round_scales[:, first:end],
+                in_=to_quantise[r][:, first * PACK : end * PACK],
             )
-            return codes, scales
+            codes[r] = round_codes
+            scales[r] = round_scales
 
-        def multiply(out, codes, scales, jj, at, cols):
+        def multiply(out, r, first_word, at, cols):
             nc.tensor.matmul_mx(
                 out=out,
-                lhsT=codes[:, jj * P : (jj + 1) * P].bitcast(FP8X4),
-                lhsT_scale=scales[:, jj * P : (jj + 1) * P],
+                lhsT=codes[r][:, first_word : first_word + P].bitcast(FP8X4),
+                lhsT_scale=scales[r][:, first_word : first_word + P],
                 rhs=w_words[:, at : at + cols].bitcast(FP8X4),
                 rhs_scale=w_scales[:, at : at + cols],
                 start=True,
                 stop=True,
             )
 
+        def multiply_x(out, i, jj, at, cols):
+            multiply(out, i - X_AHEAD, jj * P, at, cols)
+
+        def multiply_h(out, i, jj, at, cols):
+            multiply(out, i - H_AHEAD, PAIR_WORDS + jj * P, at, cols)
+
         def project(i):
             for jj in range(PAIR):
                 h_acc = bank_h.tile([P, PROJ], F32)
-                multiply(h_acc[:], x_codes[i], x_scales[i], jj, PROJ_AT, PROJ)
+                multiply_x(h_acc[:], i, jj, PROJ_AT, PROJ)
                 h_bank[i, jj] = h_acc
 
         def round_h(i, jj):
-            h_tile = h_rows.tile([P, PACK, P], BF16)
-            by_slot = h_bank[i, jj][:].rearrange("r (p t) -> r t p", t=PACK)
+            h_tile = h_rows.tile([P, 2, P, 2], BF16)
+            by_slot = h_bank[i, jj][:].rearrange("r (p u e) -> r u p e", u=2, e=2)
             if jj == 0:
                 nc.vector.tensor_copy(out=h_tile[:], in_=by_slot)
             else:
@@ -180,20 +207,23 @@ def tile_adaptiveinputsoftmax_pa_t_kernel(
             for jj in range(PAIR):
                 for t in range(PACK):
                     nc.tensor.transpose(
-                        out=ht[:, jj, t, :], in_=h_sb[i, jj][:, t, :], identity=ident_bf16[:]
+                        out=ht[:, jj, t, :],
+                        in_=h_sb[i, jj][:, t // 2, :, t % 2],
+                        identity=ident_bf16[:],
                     )
             ht_bank[i] = ht
 
         def group_h(i):
-            hg = grouped.tile([P, PAIR, P, PACK], BF16, align_bytes=64)
-            nc.scalar.copy(out=hg[:], in_=ht_bank[i][:].rearrange("p j t r -> p j r t"))
-            h_grouped[i] = hg
+            nc.scalar.copy(
+                out=values_of_h(i).rearrange("p (j r t) -> p j r t", j=PAIR, t=PACK),
+                in_=ht_bank[i][:].rearrange("p j t r -> p j r t"),
+            )
 
         def logits(i):
             for jj in range(PAIR):
                 both = bank_logits.tile([P, 2, HEAD], F32)
-                multiply(both[:, 0, :], x_codes[i], x_scales[i], jj, HEAD_AT, HEAD)
-                multiply(both[:, 1, :], h_codes[i], h_scales[i], jj, TAIL_AT, TAIL)
+                multiply_x(both[:, 0, :], i, jj, HEAD_AT, HEAD)
+                multiply_h(both[:, 1, :], i, jj, TAIL_AT, TAIL)
                 logit_bank[i, jj] = both
 
         def row_max(i):
@@ -229,10 +259,12 @@ def tile_adaptiveinputsoftmax_pa_t_kernel(
                 probs_block = result.tile([P, BLOCK, PROBS], F32)
                 probs[i // 2] = probs_block
             out_rows = probs[i // 2]
+            flat_rows = out_rows[:].rearrange("p j d -> p (j d)")
+            engine = nc.vector if i // 2 == N_BLOCKS - 1 else nc.gpsimd
             inv_sum = soft.tile([P, PAIR, 2], F32)
             nc.vector.reciprocal(out=inv_sum[:], in_=sums[i][:])
             pair_clusters = clusters[:, PAIR * i : PAIR * (i + 1), :]
-            nc.gpsimd.tensor_tensor(
+            engine.tensor_tensor(
                 out=pair_clusters,
                 in0=e[:, :, 0, HEAD_TOKENS:HEAD],
                 in1=inv_sum[:, :, 0:1].to_broadcast([P, PAIR, 2]),
@@ -240,7 +272,7 @@ def tile_adaptiveinputsoftmax_pa_t_kernel(
             )
             for jj in range(PAIR):
                 j = PAIR * (i % 2) + jj
-                nc.gpsimd.tensor_scalar(
+                engine.tensor_scalar(
                     out=out_rows[:, j, 0:HEAD_TOKENS],
                     in0=e[:, jj, 0, 0:HEAD_TOKENS],
                     scalar1=inv_sum[:, jj, 0:1],
@@ -248,7 +280,11 @@ def tile_adaptiveinputsoftmax_pa_t_kernel(
                     op0=ALU.mult,
                     op1=ALU.add,
                 )
-                nc.gpsimd.tensor_scalar(
+                if j == BLOCK - 1:
+                    nc.sync.dma_start(
+                        out=probs_blocks[i // 2][:, 0:STORE_CUT], in_=flat_rows[:, 0:STORE_CUT]
+                    )
+                engine.tensor_scalar(
                     out=out_rows[:, j, HEAD_TOKENS:PROBS],
                     in0=e[:, jj, 1, :],
                     scalar1=inv_sum[:, jj, 1:2],
@@ -258,40 +294,38 @@ def tile_adaptiveinputsoftmax_pa_t_kernel(
                 )
             if i % 2 == 1:
                 nc.sync.dma_start(
-                    out=probs_blocks[i // 2], in_=out_rows[:].rearrange("p j d -> p (j d)")
+                    out=probs_blocks[i // 2][:, STORE_CUT : BLOCK * PROBS],
+                    in_=flat_rows[:, STORE_CUT : BLOCK * PROBS],
                 )
 
-        def live(i):
-            return 0 <= i < N_PAIRS
-
-        for r in range(-4, N_PAIRS + 2):
-            if live(r + 4):
-                transpose_x(r + 4)
-            if live(r + 1):
-                transpose_h(r + 1)
-            if live(r + 3):
-                project(r + 3)
-            if live(r):
-                logits(r)
-            if live(r - 2):
-                normalise(r - 2)
-            if live(r + 4):
-                group_x(r + 4)
+        for r in range(-X_AHEAD, N_PAIRS + 2):
+            if live(r + X_AHEAD) or live(r + H_AHEAD):
+                open_round(r)
             if live(r - 1):
                 exponentials(r - 1, 0)
-            if live(r + 1):
-                group_h(r + 1)
+            if live(r + X_AHEAD):
+                transpose_x(r + X_AHEAD)
+            if live(r + H_AHEAD):
+                transpose_h(r + H_AHEAD)
+            if live(r + PROJ_AHEAD):
+                project(r + PROJ_AHEAD)
+            if live(r):
+                logits(r)
+            if live(r + X_AHEAD):
+                group_x(r + X_AHEAD)
+            if live(r + H_AHEAD):
+                group_h(r + H_AHEAD)
             if live(r - 1):
                 exponentials(r - 1, 1)
-            if live(r + 3):
-                round_h(r + 3, 0)
-                round_h(r + 3, 1)
-            if live(r + 4):
-                x_codes[r + 4], x_scales[r + 4] = quantise(x_mx, x_grouped[r + 4])
+            if live(r + PROJ_AHEAD):
+                round_h(r + PROJ_AHEAD, 0)
+                round_h(r + PROJ_AHEAD, 1)
             if live(r):
                 row_max(r)
-            if live(r + 1):
-                h_codes[r + 1], h_scales[r + 1] = quantise(h_mx, h_grouped[r + 1])
+            if live(r - 2):
+                normalise(r - 2)
+            if live(r + X_AHEAD) or live(r + H_AHEAD):
+                quantise(r)
 
         other = const.tile([P, PER_PARTITION], F32)
         nc.vector.tensor_copy(out=other[:], in_=clusters[:, :, 1])

@@ -22,12 +22,13 @@ PROJ = 512
 TAIL = 256
 PROBS = HEAD_TOKENS + TAIL
 PER_PARTITION = TOKENS // P
-BLOCK = 4
-N_BLOCKS = PER_PARTITION // BLOCK
-STORE_CUT = (BLOCK - 1) * PROBS + HEAD_TOKENS
-assert (4 * STORE_CUT) % 32 == 0 and (4 * BLOCK * PROBS) % 32 == 0
 PAIR = 2
 N_PAIRS = PER_PARTITION // PAIR
+BLOCK = 4
+N_BLOCKS = PER_PARTITION // BLOCK
+STORE_CUT = (PAIR * PROBS) // 8 * 8
+assert (4 * BLOCK * PROBS) % 32 == 0
+BLOCKS_ON_VECTOR = 2
 PAIR_WORDS = PAIR * P
 
 X_AHEAD = 5
@@ -55,8 +56,8 @@ def tile_adaptiveinputsoftmax_pa_t_kernel(
     out_1,
 ):
     nc = tc.nc
-    x_blocks = x.flatten_outer_dims().rearrange(
-        "(p s j) d -> s p (j d)", p=P, s=N_BLOCKS, j=BLOCK
+    x_pairs = x.flatten_outer_dims().rearrange(
+        "(p i j) d -> i p (j d)", p=P, i=N_PAIRS, j=PAIR
     )
     probs_blocks = out_0.flatten_outer_dims().rearrange(
         "(p s j) d -> s p (j d)", p=P, s=N_BLOCKS, j=BLOCK
@@ -65,7 +66,7 @@ def tile_adaptiveinputsoftmax_pa_t_kernel(
 
     with ExitStack() as ctx:
         const = ctx.enter_context(tc.tile_pool(name="const", bufs=1))
-        x_pool = ctx.enter_context(tc.tile_pool(name="x_pool", bufs=N_BLOCKS))
+        x_pool = ctx.enter_context(tc.tile_pool(name="x_pool", bufs=N_PAIRS))
         grouped = ctx.enter_context(tc.tile_pool(name="grouped", bufs=3))
         packed = ctx.enter_context(tc.tile_pool(name="packed", bufs=X_AHEAD + 2))
         h_rows = ctx.enter_context(tc.tile_pool(name="h_rows", bufs=3 * PAIR))
@@ -95,12 +96,10 @@ def tile_adaptiveinputsoftmax_pa_t_kernel(
 
         x_sb = {}
 
-        def load_x(s):
-            x_block = x_pool.tile([P, BLOCK, FEATURES], BF16)
-            nc.sync.dma_start(
-                out=x_block[:].rearrange("p j d -> p (j d)"), in_=x_blocks[s]
-            )
-            x_sb[s] = x_block
+        def load_x(i):
+            x_pair = x_pool.tile([P, PAIR, FEATURES], BF16)
+            nc.sync.dma_start(out=x_pair[:].rearrange("p j d -> p (j d)"), in_=x_pairs[i])
+            x_sb[i] = x_pair
 
         def load_weight(words, scales, at, cols):
             for quadrant in range(4):
@@ -116,10 +115,11 @@ def tile_adaptiveinputsoftmax_pa_t_kernel(
         load_x(0)
         load_weight(tail_proj_0_words, tail_proj_0_scales, PROJ_AT, PROJ)
         load_x(1)
+        load_x(2)
         load_weight(head_weight_words, head_weight_scales, HEAD_AT, HEAD)
         load_weight(tail_w_0_words, tail_w_0_scales, TAIL_AT, TAIL)
-        for s in range(2, N_BLOCKS):
-            load_x(s)
+        for i in range(3, N_PAIRS):
+            load_x(i)
 
         xt_bank, h_bank, h_sb, ht_bank, logit_bank = {}, {}, {}, {}, {}
         to_quantise, codes, scales = {}, {}, {}
@@ -141,8 +141,7 @@ def tile_adaptiveinputsoftmax_pa_t_kernel(
         def transpose_x(i):
             xt = bank_xt.tile([P, PAIR, 2, P], F32)
             for jj in range(PAIR):
-                c = PAIR * i + jj
-                words = x_sb[c // BLOCK][:, c % BLOCK, :].bitcast(F32)
+                words = x_sb[i][:, jj, :].bitcast(F32)
                 for u in range(2):
                     nc.tensor.transpose(
                         out=xt[:, jj, u, :],
@@ -226,17 +225,17 @@ def tile_adaptiveinputsoftmax_pa_t_kernel(
                 multiply_h(both[:, 1, :], i, jj, TAIL_AT, TAIL)
                 logit_bank[i, jj] = both
 
-        def row_max(i):
-            minus_max = soft.tile([P, PAIR, 2], F32)
-            for jj in range(PAIR):
-                nc.vector.tensor_reduce(
-                    out=minus_max[:, jj, :],
-                    in_=logit_bank[i, jj][:],
-                    axis=mybir.AxisListType.X,
-                    op=ALU.max,
-                    negate=True,
-                )
-            neg_max[i] = minus_max
+        def row_max(i, jj):
+            if jj == 0:
+                minus_max = soft.tile([P, PAIR, 2], F32)
+                neg_max[i] = minus_max
+            nc.vector.tensor_reduce(
+                out=neg_max[i][:, jj, :],
+                in_=logit_bank[i, jj][:],
+                axis=mybir.AxisListType.X,
+                op=ALU.max,
+                negate=True,
+            )
 
         def exponentials(i, jj):
             if jj == 0:
@@ -260,7 +259,7 @@ def tile_adaptiveinputsoftmax_pa_t_kernel(
                 probs[i // 2] = probs_block
             out_rows = probs[i // 2]
             flat_rows = out_rows[:].rearrange("p j d -> p (j d)")
-            engine = nc.vector if i // 2 == N_BLOCKS - 1 else nc.gpsimd
+            engine = nc.vector if i // 2 >= N_BLOCKS - BLOCKS_ON_VECTOR else nc.gpsimd
             inv_sum = soft.tile([P, PAIR, 2], F32)
             nc.vector.reciprocal(out=inv_sum[:], in_=sums[i][:])
             pair_clusters = clusters[:, PAIR * i : PAIR * (i + 1), :]
@@ -280,10 +279,6 @@ def tile_adaptiveinputsoftmax_pa_t_kernel(
                     op0=ALU.mult,
                     op1=ALU.add,
                 )
-                if j == BLOCK - 1:
-                    nc.sync.dma_start(
-                        out=probs_blocks[i // 2][:, 0:STORE_CUT], in_=flat_rows[:, 0:STORE_CUT]
-                    )
                 engine.tensor_scalar(
                     out=out_rows[:, j, HEAD_TOKENS:PROBS],
                     in0=e[:, jj, 1, :],
@@ -292,11 +287,8 @@ def tile_adaptiveinputsoftmax_pa_t_kernel(
                     op0=ALU.mult,
                     op1=ALU.mult,
                 )
-            if i % 2 == 1:
-                nc.sync.dma_start(
-                    out=probs_blocks[i // 2][:, STORE_CUT : BLOCK * PROBS],
-                    in_=flat_rows[:, STORE_CUT : BLOCK * PROBS],
-                )
+            written = slice(0, STORE_CUT) if i % 2 == 0 else slice(STORE_CUT, BLOCK * PROBS)
+            nc.sync.dma_start(out=probs_blocks[i // 2][:, written], in_=flat_rows[:, written])
 
         for r in range(-X_AHEAD, N_PAIRS + 2):
             if live(r + X_AHEAD) or live(r + H_AHEAD):
@@ -321,11 +313,13 @@ def tile_adaptiveinputsoftmax_pa_t_kernel(
                 round_h(r + PROJ_AHEAD, 0)
                 round_h(r + PROJ_AHEAD, 1)
             if live(r):
-                row_max(r)
+                row_max(r, 0)
             if live(r - 2):
                 normalise(r - 2)
             if live(r + X_AHEAD) or live(r + H_AHEAD):
                 quantise(r)
+            if live(r):
+                row_max(r, 1)
 
         other = const.tile([P, PER_PARTITION], F32)
         nc.vector.tensor_copy(out=other[:], in_=clusters[:, :, 1])

@@ -92,7 +92,7 @@ def tile_adaptiveinputsoftmax_pa_t_kernel(
         ident_bf16 = const.tile([P, P], BF16)
         make_identity(nc, ident_bf16[:])
 
-        clusters = const.tile([P, PER_PARTITION, 2], F32)
+        clusters = const.tile([P, 2, PER_PARTITION], F32)
 
         x_sb = {}
 
@@ -113,12 +113,13 @@ def tile_adaptiveinputsoftmax_pa_t_kernel(
             )
 
         load_x(0)
-        load_weight(tail_proj_0_words, tail_proj_0_scales, PROJ_AT, PROJ)
         load_x(1)
-        load_x(2)
+        load_weight(tail_proj_0_words, tail_proj_0_scales, PROJ_AT, PROJ)
+        for i in range(2, X_AHEAD + 1):
+            load_x(i)
         load_weight(head_weight_words, head_weight_scales, HEAD_AT, HEAD)
         load_weight(tail_w_0_words, tail_w_0_scales, TAIL_AT, TAIL)
-        for i in range(3, N_PAIRS):
+        for i in range(X_AHEAD + 1, N_PAIRS):
             load_x(i)
 
         xt_bank, h_bank, h_sb, ht_bank, logit_bank = {}, {}, {}, {}, {}
@@ -262,13 +263,15 @@ def tile_adaptiveinputsoftmax_pa_t_kernel(
             engine = nc.vector if i // 2 >= N_BLOCKS - BLOCKS_ON_VECTOR else nc.gpsimd
             inv_sum = soft.tile([P, PAIR, 2], F32)
             nc.vector.reciprocal(out=inv_sum[:], in_=sums[i][:])
-            pair_clusters = clusters[:, PAIR * i : PAIR * (i + 1), :]
+            pair_clusters = clusters[:, :, PAIR * i : PAIR * (i + 1)]
             engine.tensor_tensor(
                 out=pair_clusters,
-                in0=e[:, :, 0, HEAD_TOKENS:HEAD],
-                in1=inv_sum[:, :, 0:1].to_broadcast([P, PAIR, 2]),
+                in0=e[:, :, 0, HEAD_TOKENS:HEAD].rearrange("p j k -> p k j"),
+                in1=inv_sum[:, :, 0].unsqueeze(1).to_broadcast([P, 2, PAIR]),
                 op=ALU.mult,
             )
+            if i == N_PAIRS - 1:
+                nc.sync.dma_start(out=other_cluster, in_=clusters[:, 1, :])
             for jj in range(PAIR):
                 j = PAIR * (i % 2) + jj
                 engine.tensor_scalar(
@@ -283,7 +286,7 @@ def tile_adaptiveinputsoftmax_pa_t_kernel(
                     out=out_rows[:, j, HEAD_TOKENS:PROBS],
                     in0=e[:, jj, 1, :],
                     scalar1=inv_sum[:, jj, 1:2],
-                    scalar2=pair_clusters[:, jj, 0:1],
+                    scalar2=pair_clusters[:, 0, jj : jj + 1],
                     op0=ALU.mult,
                     op1=ALU.mult,
                 )
@@ -320,7 +323,3 @@ def tile_adaptiveinputsoftmax_pa_t_kernel(
                 quantise(r)
             if live(r):
                 row_max(r, 1)
-
-        other = const.tile([P, PER_PARTITION], F32)
-        nc.vector.tensor_copy(out=other[:], in_=clusters[:, :, 1])
-        nc.sync.dma_start(out=other_cluster, in_=other[:])

@@ -31,8 +31,7 @@ assert (4 * BLOCK * PROBS) % 32 == 0
 BLOCKS_ON_VECTOR = 2
 PAIR_WORDS = PAIR * P
 
-X_AHEAD = 5
-PROJ_AHEAD = 3
+X_AHEAD = 4
 H_AHEAD = 1
 
 PROJ_AT = 0
@@ -67,20 +66,20 @@ def tile_adaptiveinputsoftmax_pa_t_kernel(
     with ExitStack() as ctx:
         const = ctx.enter_context(tc.tile_pool(name="const", bufs=1))
         x_pool = ctx.enter_context(tc.tile_pool(name="x_pool", bufs=N_PAIRS))
-        grouped = ctx.enter_context(tc.tile_pool(name="grouped", bufs=3))
-        packed = ctx.enter_context(tc.tile_pool(name="packed", bufs=X_AHEAD + 2))
-        h_rows = ctx.enter_context(tc.tile_pool(name="h_rows", bufs=3 * PAIR))
+        grouped = ctx.enter_context(tc.tile_pool(name="grouped", bufs=5))
+        packed = ctx.enter_context(tc.tile_pool(name="packed", bufs=X_AHEAD + 3))
         soft = ctx.enter_context(tc.tile_pool(name="soft", bufs=4))
         result = ctx.enter_context(tc.tile_pool(name="result", bufs=3))
         bank_xt = ctx.enter_context(tc.psum_pool(name="bank_xt", bufs=2))
-        bank_ht = ctx.enter_context(tc.psum_pool(name="bank_ht", bufs=1))
-        bank_h = ctx.enter_context(tc.psum_pool(name="bank_h", bufs=PAIR))
+        bank_ht = ctx.enter_context(tc.psum_pool(name="bank_ht", bufs=3))
         bank_logits = ctx.enter_context(tc.psum_pool(name="bank_logits", bufs=3))
         ctx.enter_context(tc.manual_schedule())
 
         w_scales = const.tile([P, ALL_COLS], U8, align_bytes=64)
         nc.vector.memset(w_scales[:].bitcast(I32), 0)
         w_words = const.tile([P, ALL_COLS], U32, align_bytes=64)
+        proj_scales = const.tile([P, PROJ], U8, align_bytes=64)
+        proj_words = const.tile([P, PROJ], U32, align_bytes=64)
 
         warm_in = const.tile([P, 1], F32)
         warm_out = const.tile([P, 1], F32)
@@ -89,8 +88,6 @@ def tile_adaptiveinputsoftmax_pa_t_kernel(
 
         ident_f32 = const.tile([P, P], F32)
         make_identity(nc, ident_f32[:])
-        ident_bf16 = const.tile([P, P], BF16)
-        make_identity(nc, ident_bf16[:])
 
         clusters = const.tile([P, 2, PER_PARTITION], F32)
 
@@ -113,16 +110,25 @@ def tile_adaptiveinputsoftmax_pa_t_kernel(
             )
 
         load_x(0)
-        load_x(1)
         load_weight(tail_proj_0_words, tail_proj_0_scales, PROJ_AT, PROJ)
-        for i in range(2, X_AHEAD + 1):
+        for i in range(1, X_AHEAD):
             load_x(i)
         load_weight(head_weight_words, head_weight_scales, HEAD_AT, HEAD)
         load_weight(tail_w_0_words, tail_w_0_scales, TAIL_AT, TAIL)
-        for i in range(X_AHEAD + 1, N_PAIRS):
+        for i in range(X_AHEAD, N_PAIRS):
             load_x(i)
 
-        xt_bank, h_bank, h_sb, ht_bank, logit_bank = {}, {}, {}, {}, {}
+        def reorder_proj():
+            nc.vector.tensor_copy(
+                out=proj_words[:].bitcast(I32).rearrange("p (t m) -> p t m", t=PACK),
+                in_=w_words[:, PROJ_AT : PROJ_AT + PROJ].bitcast(I32).rearrange("p (m t) -> p t m", t=PACK),
+            )
+            nc.vector.tensor_copy(
+                out=proj_scales[:].rearrange("p (t m) -> p m t", t=PACK),
+                in_=w_scales[:, PROJ_AT : PROJ_AT + PROJ].rearrange("p (m t) -> p m t", t=PACK),
+            )
+
+        xt_bank, ht_bank, logit_bank = {}, {}, {}
         to_quantise, codes, scales = {}, {}, {}
         neg_max, exps, sums, probs = {}, {}, {}, {}
 
@@ -136,8 +142,9 @@ def tile_adaptiveinputsoftmax_pa_t_kernel(
         def values_of_x(i):
             return to_quantise[i - X_AHEAD][:, 0 : PAIR_WORDS * PACK]
 
-        def values_of_h(i):
-            return to_quantise[i - H_AHEAD][:, PAIR_WORDS * PACK : 2 * PAIR_WORDS * PACK]
+        def values_of_h(i, jj):
+            first = (PAIR_WORDS + jj * P) * PACK
+            return to_quantise[i - H_AHEAD][:, first : first + P * PACK]
 
         def transpose_x(i):
             xt = bank_xt.tile([P, PAIR, 2, P], F32)
@@ -170,60 +177,51 @@ def tile_adaptiveinputsoftmax_pa_t_kernel(
             codes[r] = round_codes
             scales[r] = round_scales
 
-        def multiply(out, r, first_word, at, cols):
-            nc.tensor.matmul_mx(
-                out=out,
-                lhsT=codes[r][:, first_word : first_word + P].bitcast(FP8X4),
-                lhsT_scale=scales[r][:, first_word : first_word + P],
-                rhs=w_words[:, at : at + cols].bitcast(FP8X4),
-                rhs_scale=w_scales[:, at : at + cols],
-                start=True,
-                stop=True,
-            )
+        def tokens_of_x(i, jj):
+            r, first = i - X_AHEAD, jj * P
+            return codes[r][:, first : first + P].bitcast(FP8X4), scales[r][:, first : first + P]
 
-        def multiply_x(out, i, jj, at, cols):
-            multiply(out, i - X_AHEAD, jj * P, at, cols)
-
-        def multiply_h(out, i, jj, at, cols):
-            multiply(out, i - H_AHEAD, PAIR_WORDS + jj * P, at, cols)
+        def tokens_of_h(i, jj):
+            r, first = i - H_AHEAD, PAIR_WORDS + jj * P
+            return codes[r][:, first : first + P].bitcast(FP8X4), scales[r][:, first : first + P]
 
         def project(i):
             for jj in range(PAIR):
-                h_acc = bank_h.tile([P, PROJ], F32)
-                multiply_x(h_acc[:], i, jj, PROJ_AT, PROJ)
-                h_bank[i, jj] = h_acc
-
-        def round_h(i, jj):
-            h_tile = h_rows.tile([P, 2, P, 2], BF16)
-            by_slot = h_bank[i, jj][:].rearrange("r (p u e) -> r u p e", u=2, e=2)
-            if jj == 0:
-                nc.vector.tensor_copy(out=h_tile[:], in_=by_slot)
-            else:
-                nc.scalar.copy(out=h_tile[:], in_=by_slot)
-            h_sb[i, jj] = h_tile
-
-        def transpose_h(i):
-            ht = bank_ht.tile([P, PAIR, PACK, P], BF16)
-            for jj in range(PAIR):
+                ht = bank_ht.tile([P, PACK, P], F32)
+                x_codes, x_scales = tokens_of_x(i, jj)
                 for t in range(PACK):
-                    nc.tensor.transpose(
-                        out=ht[:, jj, t, :],
-                        in_=h_sb[i, jj][:, t // 2, :, t % 2],
-                        identity=ident_bf16[:],
+                    nc.tensor.matmul_mx(
+                        out=ht[:, t, :],
+                        lhsT=proj_words[:, t * P : (t + 1) * P].bitcast(FP8X4),
+                        lhsT_scale=proj_scales[:, t * P : (t + 1) * P],
+                        rhs=x_codes,
+                        rhs_scale=x_scales,
+                        start=True,
+                        stop=True,
                     )
-            ht_bank[i] = ht
+                ht_bank[i, jj] = ht
 
-        def group_h(i):
+        def group_h(i, jj):
             nc.scalar.copy(
-                out=values_of_h(i).rearrange("p (j r t) -> p j r t", j=PAIR, t=PACK),
-                in_=ht_bank[i][:].rearrange("p j t r -> p j r t"),
+                out=values_of_h(i, jj).rearrange("p (r t) -> p r t", t=PACK),
+                in_=ht_bank[i, jj][:].rearrange("p t r -> p r t"),
             )
 
         def logits(i):
             for jj in range(PAIR):
                 both = bank_logits.tile([P, 2, HEAD], F32)
-                multiply_x(both[:, 0, :], i, jj, HEAD_AT, HEAD)
-                multiply_h(both[:, 1, :], i, jj, TAIL_AT, TAIL)
+                for half, (tokens, at) in enumerate(
+                    ((tokens_of_x(i, jj), HEAD_AT), (tokens_of_h(i, jj), TAIL_AT))
+                ):
+                    nc.tensor.matmul_mx(
+                        out=both[:, half, :],
+                        lhsT=tokens[0],
+                        lhsT_scale=tokens[1],
+                        rhs=w_words[:, at : at + HEAD].bitcast(FP8X4),
+                        rhs_scale=w_scales[:, at : at + HEAD],
+                        start=True,
+                        stop=True,
+                    )
                 logit_bank[i, jj] = both
 
         def row_max(i, jj):
@@ -293,33 +291,39 @@ def tile_adaptiveinputsoftmax_pa_t_kernel(
             written = slice(0, STORE_CUT) if i % 2 == 0 else slice(STORE_CUT, BLOCK * PROBS)
             nc.sync.dma_start(out=probs_blocks[i // 2][:, written], in_=flat_rows[:, written])
 
-        for r in range(-X_AHEAD, N_PAIRS + 2):
-            if live(r + X_AHEAD) or live(r + H_AHEAD):
+        def quantises(r):
+            return live(r + X_AHEAD) or live(r + H_AHEAD)
+
+        FIRST_ROUND = -X_AHEAD - 1
+        for r in (FIRST_ROUND, FIRST_ROUND + 1):
+            if quantises(r):
                 open_round(r)
-            if live(r - 1):
-                exponentials(r - 1, 0)
-            if live(r + X_AHEAD):
-                transpose_x(r + X_AHEAD)
-            if live(r + H_AHEAD):
-                transpose_h(r + H_AHEAD)
-            if live(r + PROJ_AHEAD):
-                project(r + PROJ_AHEAD)
-            if live(r):
-                logits(r)
-            if live(r + X_AHEAD):
-                group_x(r + X_AHEAD)
-            if live(r + H_AHEAD):
-                group_h(r + H_AHEAD)
-            if live(r - 1):
-                exponentials(r - 1, 1)
-            if live(r + PROJ_AHEAD):
-                round_h(r + PROJ_AHEAD, 0)
-                round_h(r + PROJ_AHEAD, 1)
-            if live(r):
-                row_max(r, 0)
-            if live(r - 2):
-                normalise(r - 2)
-            if live(r + X_AHEAD) or live(r + H_AHEAD):
+        for r in range(FIRST_ROUND, N_PAIRS + 1):
+            if quantises(r + 2):
+                open_round(r + 2)
+            if quantises(r):
                 quantise(r)
+            if live(r - 1):
+                normalise(r - 1)
+            if live(r):
+                exponentials(r, 0)
+            if live(r + X_AHEAD + 1):
+                transpose_x(r + X_AHEAD + 1)
             if live(r):
                 row_max(r, 1)
+            if live(r + 1):
+                logits(r + 1)
+            if live(r + 3):
+                group_h(r + 3, 0)
+            if live(r + X_AHEAD):
+                project(r + X_AHEAD)
+            if live(r + X_AHEAD + 1):
+                group_x(r + X_AHEAD + 1)
+            if r == FIRST_ROUND:
+                reorder_proj()
+            if live(r):
+                exponentials(r, 1)
+            if live(r + 3):
+                group_h(r + 3, 1)
+            if live(r + 1):
+                row_max(r + 1, 0)

@@ -29,6 +29,7 @@ N_BLOCKS = PER_PARTITION // BLOCK
 STORE_CUT = (PAIR * PROBS) // 8 * 8
 assert (4 * BLOCK * PROBS) % 32 == 0
 BLOCKS_ON_VECTOR = 2
+VECTOR_TAKES_H = 3
 PAIR_WORDS = PAIR * P
 
 X_AHEAD = 4
@@ -130,7 +131,7 @@ def tile_adaptiveinputsoftmax_pa_t_kernel(
 
         xt_bank, ht_bank, logit_bank = {}, {}, {}
         to_quantise, codes, scales = {}, {}, {}
-        neg_max, exps, sums, probs = {}, {}, {}, {}
+        neg_max, exps, sums, probs, inv_sum, finish = {}, {}, {}, {}, {}, {}
 
         def live(i):
             return 0 <= i < N_PAIRS
@@ -202,7 +203,8 @@ def tile_adaptiveinputsoftmax_pa_t_kernel(
                 ht_bank[i, jj] = ht
 
         def group_h(i, jj):
-            nc.scalar.copy(
+            copy = nc.vector.tensor_copy if jj == 1 and i % VECTOR_TAKES_H == 0 else nc.scalar.copy
+            copy(
                 out=values_of_h(i, jj).rearrange("p (r t) -> p r t", t=PACK),
                 in_=ht_bank[i, jj][:].rearrange("p t r -> p r t"),
             )
@@ -251,43 +253,65 @@ def tile_adaptiveinputsoftmax_pa_t_kernel(
                     accum_out=sums[i][:, jj, half : half + 1],
                 )
 
+        def reciprocals(i):
+            inv = soft.tile([P, PAIR, 2], F32)
+            nc.vector.reciprocal(out=inv[:], in_=sums[i][:])
+            inv_sum[i] = inv
+
         def normalise(i):
             e = exps[i]
+            inv = inv_sum[i]
             if i % 2 == 0:
                 probs_block = result.tile([P, BLOCK, PROBS], F32)
                 probs[i // 2] = probs_block
             out_rows = probs[i // 2]
             flat_rows = out_rows[:].rearrange("p j d -> p (j d)")
-            engine = nc.vector if i // 2 >= N_BLOCKS - BLOCKS_ON_VECTOR else nc.gpsimd
-            inv_sum = soft.tile([P, PAIR, 2], F32)
-            nc.vector.reciprocal(out=inv_sum[:], in_=sums[i][:])
+            on_vector = i // 2 >= N_BLOCKS - BLOCKS_ON_VECTOR
+            engine = nc.vector if on_vector else nc.gpsimd
             pair_clusters = clusters[:, :, PAIR * i : PAIR * (i + 1)]
-            engine.tensor_tensor(
+            nc.vector.tensor_tensor(
                 out=pair_clusters,
                 in0=e[:, :, 0, HEAD_TOKENS:HEAD].rearrange("p j k -> p k j"),
-                in1=inv_sum[:, :, 0].unsqueeze(1).to_broadcast([P, 2, PAIR]),
+                in1=inv[:, :, 0].unsqueeze(1).to_broadcast([P, 2, PAIR]),
                 op=ALU.mult,
             )
             if i == N_PAIRS - 1:
                 nc.sync.dma_start(out=other_cluster, in_=clusters[:, 1, :])
-            for jj in range(PAIR):
-                j = PAIR * (i % 2) + jj
+
+            def head(jj, by_scalar):
+                out = out_rows[:, PAIR * (i % 2) + jj, 0:HEAD_TOKENS]
+                if by_scalar:
+                    nc.scalar.activation(
+                        out=out, in_=e[:, jj, 0, 0:HEAD_TOKENS], func=ACT.Copy, scale=inv[:, jj, 0:1]
+                    )
+                else:
+                    engine.tensor_scalar(
+                        out=out,
+                        in0=e[:, jj, 0, 0:HEAD_TOKENS],
+                        scalar1=inv[:, jj, 0:1],
+                        scalar2=0.0,
+                        op0=ALU.mult,
+                        op1=ALU.add,
+                    )
+
+            def tail(jj):
                 engine.tensor_scalar(
-                    out=out_rows[:, j, 0:HEAD_TOKENS],
-                    in0=e[:, jj, 0, 0:HEAD_TOKENS],
-                    scalar1=inv_sum[:, jj, 0:1],
-                    scalar2=0.0,
-                    op0=ALU.mult,
-                    op1=ALU.add,
-                )
-                engine.tensor_scalar(
-                    out=out_rows[:, j, HEAD_TOKENS:PROBS],
+                    out=out_rows[:, PAIR * (i % 2) + jj, HEAD_TOKENS:PROBS],
                     in0=e[:, jj, 1, :],
-                    scalar1=inv_sum[:, jj, 1:2],
+                    scalar1=inv[:, jj, 1:2],
                     scalar2=pair_clusters[:, 0, jj : jj + 1],
                     op0=ALU.mult,
                     op1=ALU.mult,
                 )
+
+            tail(0)
+            tail(1)
+            head(0, False)
+            finish[i] = (head, on_vector, flat_rows)
+
+        def finish_normalise(i):
+            head, on_vector, flat_rows = finish[i]
+            head(1, not on_vector)
             written = slice(0, STORE_CUT) if i % 2 == 0 else slice(STORE_CUT, BLOCK * PROBS)
             nc.sync.dma_start(out=probs_blocks[i // 2][:, written], in_=flat_rows[:, written])
 
@@ -301,6 +325,8 @@ def tile_adaptiveinputsoftmax_pa_t_kernel(
         for r in range(FIRST_ROUND, N_PAIRS + 1):
             if quantises(r + 2):
                 open_round(r + 2)
+            if live(r - 1):
+                reciprocals(r - 1)
             if quantises(r):
                 quantise(r)
             if live(r - 1):
@@ -315,6 +341,8 @@ def tile_adaptiveinputsoftmax_pa_t_kernel(
                 logits(r + 1)
             if live(r + 3):
                 group_h(r + 3, 0)
+            if live(r - 1):
+                finish_normalise(r - 1)
             if live(r + X_AHEAD):
                 project(r + X_AHEAD)
             if live(r + X_AHEAD + 1):

@@ -322,6 +322,7 @@ def tile_adaptiveinputsoftmax_pa_t_kernel(
         for r in (FIRST_ROUND, FIRST_ROUND + 1):
             if quantises(r):
                 open_round(r)
+        transpose_x(0)
         for r in range(FIRST_ROUND, N_PAIRS + 1):
             if quantises(r + 2):
                 open_round(r + 2)
@@ -333,8 +334,6 @@ def tile_adaptiveinputsoftmax_pa_t_kernel(
                 normalise(r - 1)
             if live(r):
                 exponentials(r, 0)
-            if live(r + X_AHEAD + 1):
-                transpose_x(r + X_AHEAD + 1)
             if live(r):
                 row_max(r, 1)
             if live(r + 1):
@@ -343,6 +342,8 @@ def tile_adaptiveinputsoftmax_pa_t_kernel(
                 group_h(r + 3, 0)
             if live(r - 1):
                 finish_normalise(r - 1)
+            if live(r + X_AHEAD + 2):
+                transpose_x(r + X_AHEAD + 2)
             if live(r + X_AHEAD):
                 project(r + X_AHEAD)
             if live(r + X_AHEAD + 1):

@@ -26,10 +26,9 @@ PAIR = 2
 N_PAIRS = PER_PARTITION // PAIR
 BLOCK = 4
 N_BLOCKS = PER_PARTITION // BLOCK
-STORE_CUT = (PAIR * PROBS) // 8 * 8
 assert (4 * BLOCK * PROBS) % 32 == 0
-BLOCKS_ON_VECTOR = 2
-VECTOR_TAKES_H = 3
+VECTOR_TAKES_H = 4
+EARLY_PAIRS = (1, 2)
 PAIR_WORDS = PAIR * P
 
 X_AHEAD = 4
@@ -131,7 +130,7 @@ def tile_adaptiveinputsoftmax_pa_t_kernel(
 
         xt_bank, ht_bank, logit_bank = {}, {}, {}
         to_quantise, codes, scales = {}, {}, {}
-        neg_max, exps, sums, probs, inv_sum, finish = {}, {}, {}, {}, {}, {}
+        neg_max, exps, sums, probs, inv_sum = {}, {}, {}, {}, {}
 
         def live(i):
             return 0 <= i < N_PAIRS
@@ -160,7 +159,8 @@ def tile_adaptiveinputsoftmax_pa_t_kernel(
             xt_bank[i] = xt
 
         def group_x(i):
-            nc.vector.tensor_copy(
+            copy = nc.scalar.copy if i in EARLY_PAIRS else nc.vector.tensor_copy
+            copy(
                 out=values_of_x(i).bitcast(F32).rearrange("p (j r u) -> p j r u", j=PAIR, u=2),
                 in_=xt_bank[i][:].rearrange("p j u r -> p j r u"),
             )
@@ -202,8 +202,12 @@ def tile_adaptiveinputsoftmax_pa_t_kernel(
                     )
                 ht_bank[i, jj] = ht
 
+        def vector_takes_h(i):
+            return live(i) and (i % VECTOR_TAKES_H == 0 or i >= N_PAIRS - 2)
+
         def group_h(i, jj):
-            copy = nc.vector.tensor_copy if jj == 1 and i % VECTOR_TAKES_H == 0 else nc.scalar.copy
+            by_vector = jj == 1 and vector_takes_h(i)
+            copy = nc.vector.tensor_copy if by_vector else nc.scalar.copy
             copy(
                 out=values_of_h(i, jj).rearrange("p (r t) -> p r t", t=PACK),
                 in_=ht_bank[i, jj][:].rearrange("p t r -> p r t"),
@@ -258,61 +262,44 @@ def tile_adaptiveinputsoftmax_pa_t_kernel(
             nc.vector.reciprocal(out=inv[:], in_=sums[i][:])
             inv_sum[i] = inv
 
-        def normalise(i):
-            e = exps[i]
-            inv = inv_sum[i]
+        def cluster_probabilities(i):
             if i % 2 == 0:
                 probs_block = result.tile([P, BLOCK, PROBS], F32)
                 probs[i // 2] = probs_block
-            out_rows = probs[i // 2]
-            flat_rows = out_rows[:].rearrange("p j d -> p (j d)")
-            on_vector = i // 2 >= N_BLOCKS - BLOCKS_ON_VECTOR
-            engine = nc.vector if on_vector else nc.gpsimd
-            pair_clusters = clusters[:, :, PAIR * i : PAIR * (i + 1)]
             nc.vector.tensor_tensor(
-                out=pair_clusters,
-                in0=e[:, :, 0, HEAD_TOKENS:HEAD].rearrange("p j k -> p k j"),
-                in1=inv[:, :, 0].unsqueeze(1).to_broadcast([P, 2, PAIR]),
+                out=clusters[:, :, PAIR * i : PAIR * (i + 1)],
+                in0=exps[i][:, :, 0, HEAD_TOKENS:HEAD].rearrange("p j k -> p k j"),
+                in1=inv_sum[i][:, :, 0].unsqueeze(1).to_broadcast([P, 2, PAIR]),
                 op=ALU.mult,
             )
             if i == N_PAIRS - 1:
                 nc.sync.dma_start(out=other_cluster, in_=clusters[:, 1, :])
 
-            def head(jj, by_scalar):
-                out = out_rows[:, PAIR * (i % 2) + jj, 0:HEAD_TOKENS]
-                if by_scalar:
-                    nc.scalar.activation(
-                        out=out, in_=e[:, jj, 0, 0:HEAD_TOKENS], func=ACT.Copy, scale=inv[:, jj, 0:1]
-                    )
-                else:
-                    engine.tensor_scalar(
-                        out=out,
-                        in0=e[:, jj, 0, 0:HEAD_TOKENS],
-                        scalar1=inv[:, jj, 0:1],
-                        scalar2=0.0,
-                        op0=ALU.mult,
-                        op1=ALU.add,
-                    )
-
-            def tail(jj):
+        def scale_head(i, jj, engine):
+            out = probs[i // 2][:, PAIR * (i % 2) + jj, 0:HEAD_TOKENS]
+            e_head = exps[i][:, jj, 0, 0:HEAD_TOKENS]
+            factor = inv_sum[i][:, jj, 0:1]
+            if engine is None:
+                nc.scalar.activation(out=out, in_=e_head, func=ACT.Copy, scale=factor)
+            else:
                 engine.tensor_scalar(
-                    out=out_rows[:, PAIR * (i % 2) + jj, HEAD_TOKENS:PROBS],
-                    in0=e[:, jj, 1, :],
-                    scalar1=inv[:, jj, 1:2],
-                    scalar2=pair_clusters[:, 0, jj : jj + 1],
-                    op0=ALU.mult,
-                    op1=ALU.mult,
+                    out=out, in0=e_head, scalar1=factor, scalar2=0.0, op0=ALU.mult, op1=ALU.add
                 )
 
-            tail(0)
-            tail(1)
-            head(0, False)
-            finish[i] = (head, on_vector, flat_rows)
+        def scale_tail(i, jj, engine):
+            engine.tensor_scalar(
+                out=probs[i // 2][:, PAIR * (i % 2) + jj, HEAD_TOKENS:PROBS],
+                in0=exps[i][:, jj, 1, :],
+                scalar1=inv_sum[i][:, jj, 1:2],
+                scalar2=clusters[:, 0, PAIR * i + jj : PAIR * i + jj + 1],
+                op0=ALU.mult,
+                op1=ALU.mult,
+            )
 
-        def finish_normalise(i):
-            head, on_vector, flat_rows = finish[i]
-            head(1, not on_vector)
-            written = slice(0, STORE_CUT) if i % 2 == 0 else slice(STORE_CUT, BLOCK * PROBS)
+        def store(i, first_tile, tiles):
+            j = PAIR * (i % 2) + first_tile
+            written = slice(j * PROBS // 8 * 8, (j + tiles) * PROBS // 8 * 8)
+            flat_rows = probs[i // 2][:].rearrange("p j d -> p (j d)")
             nc.sync.dma_start(out=probs_blocks[i // 2][:, written], in_=flat_rows[:, written])
 
         def quantises(r):
@@ -324,24 +311,36 @@ def tile_adaptiveinputsoftmax_pa_t_kernel(
                 open_round(r)
         transpose_x(0)
         for r in range(FIRST_ROUND, N_PAIRS + 1):
+            done = r - 1
+            in_last_block = done >= N_PAIRS - 2
             if quantises(r + 2):
                 open_round(r + 2)
-            if live(r - 1):
-                reciprocals(r - 1)
+            if in_last_block and live(r):
+                row_max(r, 1)
+            if live(done):
+                reciprocals(done)
             if quantises(r):
                 quantise(r)
-            if live(r - 1):
-                normalise(r - 1)
+            if live(done):
+                cluster_probabilities(done)
+                if not in_last_block:
+                    scale_tail(done, 0, nc.gpsimd)
+                    scale_tail(done, 1, nc.gpsimd)
+                    scale_head(done, 0, nc.gpsimd)
+                    if vector_takes_h(r + 3):
+                        scale_head(done, 1, nc.gpsimd)
             if live(r):
                 exponentials(r, 0)
-            if live(r):
+            if live(r) and not in_last_block:
                 row_max(r, 1)
             if live(r + 1):
                 logits(r + 1)
             if live(r + 3):
                 group_h(r + 3, 0)
-            if live(r - 1):
-                finish_normalise(r - 1)
+            if live(done) and not in_last_block:
+                if not vector_takes_h(r + 3):
+                    scale_head(done, 1, None)
+                store(done, 0, PAIR)
             if live(r + X_AHEAD + 2):
                 transpose_x(r + X_AHEAD + 2)
             if live(r + X_AHEAD):
@@ -352,6 +351,11 @@ def tile_adaptiveinputsoftmax_pa_t_kernel(
                 reorder_proj()
             if live(r):
                 exponentials(r, 1)
+            if live(done) and in_last_block:
+                for jj in range(PAIR):
+                    scale_tail(done, jj, nc.vector)
+                    scale_head(done, jj, None if live(r) else nc.vector)
+                    store(done, jj, 1)
             if live(r + 3):
                 group_h(r + 3, 1)
             if live(r + 1):

@@ -27,8 +27,9 @@ N_PAIRS = PER_PARTITION // PAIR
 BLOCK = 4
 N_BLOCKS = PER_PARTITION // BLOCK
 assert (4 * BLOCK * PROBS) % 32 == 0
-VECTOR_TAKES_H = 4
+VECTOR_TAKES_H = 5
 EARLY_PAIRS = (1, 2)
+CLOSING_PAIRS = 4
 PAIR_WORDS = PAIR * P
 
 X_AHEAD = 4
@@ -68,7 +69,7 @@ def tile_adaptiveinputsoftmax_pa_t_kernel(
         x_pool = ctx.enter_context(tc.tile_pool(name="x_pool", bufs=N_PAIRS))
         grouped = ctx.enter_context(tc.tile_pool(name="grouped", bufs=5))
         packed = ctx.enter_context(tc.tile_pool(name="packed", bufs=X_AHEAD + 3))
-        soft = ctx.enter_context(tc.tile_pool(name="soft", bufs=4))
+        soft = ctx.enter_context(tc.tile_pool(name="soft", bufs=6))
         result = ctx.enter_context(tc.tile_pool(name="result", bufs=3))
         bank_xt = ctx.enter_context(tc.psum_pool(name="bank_xt", bufs=2))
         bank_ht = ctx.enter_context(tc.psum_pool(name="bank_ht", bufs=3))
@@ -311,36 +312,39 @@ def tile_adaptiveinputsoftmax_pa_t_kernel(
                 open_round(r)
         transpose_x(0)
         for r in range(FIRST_ROUND, N_PAIRS + 1):
-            done = r - 1
-            in_last_block = done >= N_PAIRS - 2
+            settled = r - 2 if 0 <= r - 2 < N_PAIRS - CLOSING_PAIRS else None
+            closing = r - 1 if N_PAIRS - CLOSING_PAIRS <= r - 1 < N_PAIRS else None
             if quantises(r + 2):
                 open_round(r + 2)
-            if in_last_block and live(r):
+            if closing is not None and live(r):
                 row_max(r, 1)
-            if live(done):
-                reciprocals(done)
+            if settled is not None:
+                reciprocals(settled)
+            if closing is not None:
+                reciprocals(closing)
             if quantises(r):
                 quantise(r)
-            if live(done):
-                cluster_probabilities(done)
-                if not in_last_block:
-                    scale_tail(done, 0, nc.gpsimd)
-                    scale_tail(done, 1, nc.gpsimd)
-                    scale_head(done, 0, nc.gpsimd)
-                    if vector_takes_h(r + 3):
-                        scale_head(done, 1, nc.gpsimd)
+            if settled is not None:
+                cluster_probabilities(settled)
+                scale_tail(settled, 0, nc.gpsimd)
+                scale_tail(settled, 1, nc.gpsimd)
+                scale_head(settled, 0, nc.gpsimd)
+                if vector_takes_h(r + 3):
+                    scale_head(settled, 1, nc.gpsimd)
+            if closing is not None:
+                cluster_probabilities(closing)
             if live(r):
                 exponentials(r, 0)
-            if live(r) and not in_last_block:
+            if live(r) and closing is None:
                 row_max(r, 1)
             if live(r + 1):
                 logits(r + 1)
             if live(r + 3):
                 group_h(r + 3, 0)
-            if live(done) and not in_last_block:
+            if settled is not None:
                 if not vector_takes_h(r + 3):
-                    scale_head(done, 1, None)
-                store(done, 0, PAIR)
+                    scale_head(settled, 1, None)
+                store(settled, 0, PAIR)
             if live(r + X_AHEAD + 2):
                 transpose_x(r + X_AHEAD + 2)
             if live(r + X_AHEAD):
@@ -351,12 +355,14 @@ def tile_adaptiveinputsoftmax_pa_t_kernel(
                 reorder_proj()
             if live(r):
                 exponentials(r, 1)
-            if live(done) and in_last_block:
+            if closing is not None:
                 for jj in range(PAIR):
-                    scale_tail(done, jj, nc.vector)
-                    scale_head(done, jj, None if live(r) else nc.vector)
-                    store(done, jj, 1)
-            if live(r + 3):
+                    scale_tail(closing, jj, nc.vector)
+                    scale_head(closing, jj, None if live(r) else nc.vector)
+                    store(closing, jj, 1)
+            if live(r + 3) and not vector_takes_h(r + 3):
                 group_h(r + 3, 1)
             if live(r + 1):
                 row_max(r + 1, 0)
+            if vector_takes_h(r + 3):
+                group_h(r + 3, 1)

@@ -69,7 +69,7 @@ def tile_adaptiveinputsoftmax_pa_t_kernel(
         x_pool = ctx.enter_context(tc.tile_pool(name="x_pool", bufs=N_PAIRS))
         grouped = ctx.enter_context(tc.tile_pool(name="grouped", bufs=5))
         packed = ctx.enter_context(tc.tile_pool(name="packed", bufs=X_AHEAD + 3))
-        soft = ctx.enter_context(tc.tile_pool(name="soft", bufs=6))
+        soft = ctx.enter_context(tc.tile_pool(name="soft", bufs=7))
         result = ctx.enter_context(tc.tile_pool(name="result", bufs=3))
         bank_xt = ctx.enter_context(tc.psum_pool(name="bank_xt", bufs=2))
         bank_ht = ctx.enter_context(tc.psum_pool(name="bank_ht", bufs=3))
@@ -311,19 +311,24 @@ def tile_adaptiveinputsoftmax_pa_t_kernel(
             if quantises(r):
                 open_round(r)
         transpose_x(0)
+        def early(i):
+            return 0 <= i < N_PAIRS - CLOSING_PAIRS
+
         for r in range(FIRST_ROUND, N_PAIRS + 1):
-            settled = r - 2 if 0 <= r - 2 < N_PAIRS - CLOSING_PAIRS else None
+            settled = r - 3 if early(r - 3) else None
             closing = r - 1 if N_PAIRS - CLOSING_PAIRS <= r - 1 < N_PAIRS else None
             if quantises(r + 2):
                 open_round(r + 2)
             if closing is not None and live(r):
                 row_max(r, 1)
-            if settled is not None:
-                reciprocals(settled)
             if closing is not None:
                 reciprocals(closing)
-            if quantises(r):
-                quantise(r)
+            if early(r - 2):
+                reciprocals(r - 2)
+            if closing is not None:
+                cluster_probabilities(closing)
+                for jj in range(PAIR):
+                    scale_tail(closing, jj, nc.vector)
             if settled is not None:
                 cluster_probabilities(settled)
                 scale_tail(settled, 0, nc.gpsimd)
@@ -331,8 +336,8 @@ def tile_adaptiveinputsoftmax_pa_t_kernel(
                 scale_head(settled, 0, nc.gpsimd)
                 if vector_takes_h(r + 3):
                     scale_head(settled, 1, nc.gpsimd)
-            if closing is not None:
-                cluster_probabilities(closing)
+            if quantises(r):
+                quantise(r)
             if live(r):
                 exponentials(r, 0)
             if live(r) and closing is None:
@@ -357,7 +362,6 @@ def tile_adaptiveinputsoftmax_pa_t_kernel(
                 exponentials(r, 1)
             if closing is not None:
                 for jj in range(PAIR):
-                    scale_tail(closing, jj, nc.vector)
                     scale_head(closing, jj, None if live(r) else nc.vector)
                     store(closing, jj, 1)
             if live(r + 3) and not vector_takes_h(r + 3):

@@ -319,16 +319,8 @@ def tile_adaptiveinputsoftmax_pa_t_kernel(
             closing = r - 1 if N_PAIRS - CLOSING_PAIRS <= r - 1 < N_PAIRS else None
             if quantises(r + 2):
                 open_round(r + 2)
-            if closing is not None and live(r):
-                row_max(r, 1)
-            if closing is not None:
-                reciprocals(closing)
             if early(r - 2):
                 reciprocals(r - 2)
-            if closing is not None:
-                cluster_probabilities(closing)
-                for jj in range(PAIR):
-                    scale_tail(closing, jj, nc.vector)
             if settled is not None:
                 cluster_probabilities(settled)
                 scale_tail(settled, 0, nc.gpsimd)
@@ -340,7 +332,7 @@ def tile_adaptiveinputsoftmax_pa_t_kernel(
                 quantise(r)
             if live(r):
                 exponentials(r, 0)
-            if live(r) and closing is None:
+            if live(r):
                 row_max(r, 1)
             if live(r + 1):
                 logits(r + 1)
@@ -360,13 +352,16 @@ def tile_adaptiveinputsoftmax_pa_t_kernel(
                 reorder_proj()
             if live(r):
                 exponentials(r, 1)
-            if closing is not None:
-                for jj in range(PAIR):
-                    scale_head(closing, jj, None if live(r) else nc.vector)
-                    store(closing, jj, 1)
             if live(r + 3) and not vector_takes_h(r + 3):
                 group_h(r + 3, 1)
             if live(r + 1):
                 row_max(r + 1, 0)
             if vector_takes_h(r + 3):
                 group_h(r + 3, 1)
+            if closing is not None:
+                reciprocals(closing)
+                cluster_probabilities(closing)
+                for jj in range(PAIR):
+                    scale_tail(closing, jj, nc.vector)
+                    scale_head(closing, jj, None if live(r) else nc.vector)
+                    store(closing, jj, 1)

@@ -27,7 +27,7 @@ N_PAIRS = PER_PARTITION // PAIR
 BLOCK = 4
 N_BLOCKS = PER_PARTITION // BLOCK
 assert (4 * BLOCK * PROBS) % 32 == 0
-VECTOR_TAKES_H = 5
+VECTOR_TAKES_H = 4
 EARLY_PAIRS = (1, 2)
 CLOSING_PAIRS = 4
 PAIR_WORDS = PAIR * P
@@ -111,8 +111,9 @@ def tile_adaptiveinputsoftmax_pa_t_kernel(
             )
 
         load_x(0)
+        load_x(1)
         load_weight(tail_proj_0_words, tail_proj_0_scales, PROJ_AT, PROJ)
-        for i in range(1, X_AHEAD):
+        for i in range(2, X_AHEAD):
             load_x(i)
         load_weight(head_weight_words, head_weight_scales, HEAD_AT, HEAD)
         load_weight(tail_w_0_words, tail_w_0_scales, TAIL_AT, TAIL)
@@ -204,7 +205,7 @@ def tile_adaptiveinputsoftmax_pa_t_kernel(
                 ht_bank[i, jj] = ht
 
         def vector_takes_h(i):
-            return live(i) and (i % VECTOR_TAKES_H == 0 or i >= N_PAIRS - 2)
+            return live(i) and (i % VECTOR_TAKES_H == VECTOR_TAKES_H - 1 or i >= N_PAIRS - 2)
 
         def group_h(i, jj):
             by_vector = jj == 1 and vector_takes_h(i)
@@ -319,6 +320,8 @@ def tile_adaptiveinputsoftmax_pa_t_kernel(
             closing = r - 1 if N_PAIRS - CLOSING_PAIRS <= r - 1 < N_PAIRS else None
             if quantises(r + 2):
                 open_round(r + 2)
+            if r + X_AHEAD + 1 in EARLY_PAIRS:
+                group_x(r + X_AHEAD + 1)
             if early(r - 2):
                 reciprocals(r - 2)
             if settled is not None:
@@ -346,7 +349,7 @@ def tile_adaptiveinputsoftmax_pa_t_kernel(
                 transpose_x(r + X_AHEAD + 2)
             if live(r + X_AHEAD):
                 project(r + X_AHEAD)
-            if live(r + X_AHEAD + 1):
+            if live(r + X_AHEAD + 1) and r + X_AHEAD + 1 not in EARLY_PAIRS:
                 group_x(r + X_AHEAD + 1)
             if r == FIRST_ROUND:
                 reorder_proj()

@@ -27,9 +27,8 @@ N_PAIRS = PER_PARTITION // PAIR
 BLOCK = 4
 N_BLOCKS = PER_PARTITION // BLOCK
 assert (4 * BLOCK * PROBS) % 32 == 0
-VECTOR_TAKES_H = 4
-EARLY_PAIRS = (1, 2)
-CLOSING_PAIRS = 4
+SCALAR_TAKES_X = (10, 20)
+CLOSING_PAIRS = 3
 PAIR_WORDS = PAIR * P
 
 X_AHEAD = 4
@@ -77,7 +76,8 @@ def tile_adaptiveinputsoftmax_pa_t_kernel(
         ctx.enter_context(tc.manual_schedule())
 
         w_scales = const.tile([P, ALL_COLS], U8, align_bytes=64)
-        nc.vector.memset(w_scales[:].bitcast(I32), 0)
+        for first, end in ((PROJ_AT, PROJ_AT + PROJ), (HEAD_AT, ALL_COLS)):
+            nc.vector.memset(w_scales[:, first:end].bitcast(I32), 0)
         w_words = const.tile([P, ALL_COLS], U32, align_bytes=64)
         proj_scales = const.tile([P, PROJ], U8, align_bytes=64)
         proj_words = const.tile([P, PROJ], U32, align_bytes=64)
@@ -96,7 +96,11 @@ def tile_adaptiveinputsoftmax_pa_t_kernel(
 
         def load_x(i):
             x_pair = x_pool.tile([P, PAIR, FEATURES], BF16)
-            nc.sync.dma_start(out=x_pair[:].rearrange("p j d -> p (j d)"), in_=x_pairs[i])
+            flat = x_pair[:].rearrange("p j d -> p (j d)")
+            width = FEATURES if i == 0 else PAIR * FEATURES
+            for first in range(0, PAIR * FEATURES, width):
+                cols = slice(first, first + width)
+                nc.sync.dma_start(out=flat[:, cols], in_=x_pairs[i][:, cols])
             x_sb[i] = x_pair
 
         def load_weight(words, scales, at, cols):
@@ -111,13 +115,14 @@ def tile_adaptiveinputsoftmax_pa_t_kernel(
             )
 
         load_x(0)
-        load_x(1)
         load_weight(tail_proj_0_words, tail_proj_0_scales, PROJ_AT, PROJ)
-        for i in range(2, X_AHEAD):
+        for i in range(1, 5):
             load_x(i)
         load_weight(head_weight_words, head_weight_scales, HEAD_AT, HEAD)
+        for i in range(5, 5):
+            load_x(i)
         load_weight(tail_w_0_words, tail_w_0_scales, TAIL_AT, TAIL)
-        for i in range(X_AHEAD, N_PAIRS):
+        for i in range(5, N_PAIRS):
             load_x(i)
 
         def reorder_proj():
@@ -149,8 +154,9 @@ def tile_adaptiveinputsoftmax_pa_t_kernel(
             return to_quantise[i - H_AHEAD][:, first : first + P * PACK]
 
         def transpose_x(i):
-            xt = bank_xt.tile([P, PAIR, 2, P], F32)
             for jj in range(PAIR):
+                if jj == 0 or i == 0:
+                    xt = bank_xt.tile([P, PAIR, 2, P], F32)
                 words = x_sb[i][:, jj, :].bitcast(F32)
                 for u in range(2):
                     nc.tensor.transpose(
@@ -158,14 +164,19 @@ def tile_adaptiveinputsoftmax_pa_t_kernel(
                         in_=words[:, u : FEATURES // 2 : 2],
                         identity=ident_f32[:],
                     )
-            xt_bank[i] = xt
+                xt_bank[i, jj] = xt
 
         def group_x(i):
-            copy = nc.scalar.copy if i in EARLY_PAIRS else nc.vector.tensor_copy
-            copy(
-                out=values_of_x(i).bitcast(F32).rearrange("p (j r u) -> p j r u", j=PAIR, u=2),
-                in_=xt_bank[i][:].rearrange("p j u r -> p j r u"),
-            )
+            words = values_of_x(i).bitcast(F32).rearrange("p (j r u) -> p j r u", j=PAIR, u=2)
+            if i == 0:
+                for jj, copy in enumerate((nc.vector.tensor_copy, nc.scalar.copy)):
+                    copy(
+                        out=words[:, jj, :, :],
+                        in_=xt_bank[i, jj][:, jj, :, :].rearrange("p u r -> p r u"),
+                    )
+            else:
+                copy = nc.scalar.copy if i in SCALAR_TAKES_X else nc.vector.tensor_copy
+                copy(out=words, in_=xt_bank[i, 0][:].rearrange("p j u r -> p j r u"))
 
         def quantise(r):
             round_codes = packed.tile([P, 2 * PAIR_WORDS], U32, align_bytes=64)
@@ -204,13 +215,8 @@ def tile_adaptiveinputsoftmax_pa_t_kernel(
                     )
                 ht_bank[i, jj] = ht
 
-        def vector_takes_h(i):
-            return live(i) and (i % VECTOR_TAKES_H == VECTOR_TAKES_H - 1 or i >= N_PAIRS - 2)
-
         def group_h(i, jj):
-            by_vector = jj == 1 and vector_takes_h(i)
-            copy = nc.vector.tensor_copy if by_vector else nc.scalar.copy
-            copy(
+            nc.scalar.copy(
                 out=values_of_h(i, jj).rearrange("p (r t) -> p r t", t=PACK),
                 in_=ht_bank[i, jj][:].rearrange("p t r -> p r t"),
             )
@@ -259,34 +265,34 @@ def tile_adaptiveinputsoftmax_pa_t_kernel(
                     accum_out=sums[i][:, jj, half : half + 1],
                 )
 
-        def reciprocals(i):
-            inv = soft.tile([P, PAIR, 2], F32)
-            nc.vector.reciprocal(out=inv[:], in_=sums[i][:])
-            inv_sum[i] = inv
+        def reciprocals(i, tiles=slice(0, PAIR)):
+            if tiles.start == 0:
+                inv = soft.tile([P, PAIR, 2], F32)
+                inv_sum[i] = inv
+            nc.vector.reciprocal(out=inv_sum[i][:, tiles, :], in_=sums[i][:, tiles, :])
 
-        def cluster_probabilities(i):
+        def open_probs(i):
             if i % 2 == 0:
                 probs_block = result.tile([P, BLOCK, PROBS], F32)
                 probs[i // 2] = probs_block
+
+        def cluster_probabilities(i, tiles=slice(0, PAIR)):
             nc.vector.tensor_tensor(
-                out=clusters[:, :, PAIR * i : PAIR * (i + 1)],
-                in0=exps[i][:, :, 0, HEAD_TOKENS:HEAD].rearrange("p j k -> p k j"),
-                in1=inv_sum[i][:, :, 0].unsqueeze(1).to_broadcast([P, 2, PAIR]),
+                out=clusters[:, :, PAIR * i + tiles.start : PAIR * i + tiles.stop],
+                in0=exps[i][:, tiles, 0, HEAD_TOKENS:HEAD].rearrange("p j k -> p k j"),
+                in1=inv_sum[i][:, tiles, 0].unsqueeze(1).to_broadcast([P, 2, tiles.stop - tiles.start]),
                 op=ALU.mult,
             )
-            if i == N_PAIRS - 1:
+            if i == N_PAIRS - 1 and tiles.stop == PAIR:
                 nc.sync.dma_start(out=other_cluster, in_=clusters[:, 1, :])
 
         def scale_head(i, jj, engine):
             out = probs[i // 2][:, PAIR * (i % 2) + jj, 0:HEAD_TOKENS]
             e_head = exps[i][:, jj, 0, 0:HEAD_TOKENS]
             factor = inv_sum[i][:, jj, 0:1]
-            if engine is None:
-                nc.scalar.activation(out=out, in_=e_head, func=ACT.Copy, scale=factor)
-            else:
-                engine.tensor_scalar(
-                    out=out, in0=e_head, scalar1=factor, scalar2=0.0, op0=ALU.mult, op1=ALU.add
-                )
+            engine.tensor_scalar(
+                out=out, in0=e_head, scalar1=factor, scalar2=0.0, op0=ALU.mult, op1=ALU.add
+            )
 
         def scale_tail(i, jj, engine):
             engine.tensor_scalar(
@@ -312,25 +318,25 @@ def tile_adaptiveinputsoftmax_pa_t_kernel(
             if quantises(r):
                 open_round(r)
         transpose_x(0)
+
         def early(i):
             return 0 <= i < N_PAIRS - CLOSING_PAIRS
 
         for r in range(FIRST_ROUND, N_PAIRS + 1):
-            settled = r - 3 if early(r - 3) else None
+            settled = r - 2 if early(r - 2) else None
             closing = r - 1 if N_PAIRS - CLOSING_PAIRS <= r - 1 < N_PAIRS else None
             if quantises(r + 2):
                 open_round(r + 2)
-            if r + X_AHEAD + 1 in EARLY_PAIRS:
+            if live(r):
+                open_probs(r)
+            if r + X_AHEAD + 1 in SCALAR_TAKES_X:
                 group_x(r + X_AHEAD + 1)
-            if early(r - 2):
-                reciprocals(r - 2)
             if settled is not None:
+                scale_head(settled, 1, nc.vector)
                 cluster_probabilities(settled)
                 scale_tail(settled, 0, nc.gpsimd)
-                scale_tail(settled, 1, nc.gpsimd)
                 scale_head(settled, 0, nc.gpsimd)
-                if vector_takes_h(r + 3):
-                    scale_head(settled, 1, nc.gpsimd)
+                scale_tail(settled, 1, nc.gpsimd if early(settled + 1) else nc.vector)
             if quantises(r):
                 quantise(r)
             if live(r):
@@ -342,29 +348,30 @@ def tile_adaptiveinputsoftmax_pa_t_kernel(
             if live(r + 3):
                 group_h(r + 3, 0)
             if settled is not None:
-                if not vector_takes_h(r + 3):
-                    scale_head(settled, 1, None)
                 store(settled, 0, PAIR)
             if live(r + X_AHEAD + 2):
                 transpose_x(r + X_AHEAD + 2)
             if live(r + X_AHEAD):
                 project(r + X_AHEAD)
-            if live(r + X_AHEAD + 1) and r + X_AHEAD + 1 not in EARLY_PAIRS:
+            if live(r + X_AHEAD + 1) and r + X_AHEAD + 1 not in SCALAR_TAKES_X:
                 group_x(r + X_AHEAD + 1)
             if r == FIRST_ROUND:
                 reorder_proj()
             if live(r):
                 exponentials(r, 1)
-            if live(r + 3) and not vector_takes_h(r + 3):
+            if live(r + 3):
                 group_h(r + 3, 1)
+            if live(r - 1) and r - 1 < N_PAIRS - 1:
+                reciprocals(r - 1)
             if live(r + 1):
                 row_max(r + 1, 0)
-            if vector_takes_h(r + 3):
-                group_h(r + 3, 1)
             if closing is not None:
-                reciprocals(closing)
-                cluster_probabilities(closing)
-                for jj in range(PAIR):
-                    scale_tail(closing, jj, nc.vector)
-                    scale_head(closing, jj, None if live(r) else nc.vector)
-                    store(closing, jj, 1)
+                last = closing == N_PAIRS - 1
+                for tiles in ((slice(0, 1), slice(1, 2)) if last else (slice(0, PAIR),)):
+                    if last:
+                        reciprocals(closing, tiles)
+                    cluster_probabilities(closing, tiles)
+                    for jj in range(tiles.start, tiles.stop):
+                        scale_tail(closing, jj, nc.vector)
+                        scale_head(closing, jj, nc.vector)
+                        store(closing, jj, 1)

@@ -310,6 +310,15 @@ def tile_adaptiveinputsoftmax_pa_t_kernel(
             flat_rows = probs[i // 2][:].rearrange("p j d -> p (j d)")
             nc.sync.dma_start(out=probs_blocks[i // 2][:, written], in_=flat_rows[:, written])
 
+        def statistics(i, tiles=slice(0, PAIR)):
+            reciprocals(i, tiles)
+            cluster_probabilities(i, tiles)
+
+        def finish(i, jj):
+            scale_head(i, jj, nc.vector)
+            scale_tail(i, jj, nc.vector)
+            store(i, jj, 1)
+
         def quantises(r):
             return live(r + X_AHEAD) or live(r + H_AHEAD)
 
@@ -336,11 +345,16 @@ def tile_adaptiveinputsoftmax_pa_t_kernel(
                 cluster_probabilities(settled)
                 scale_tail(settled, 0, nc.gpsimd)
                 scale_head(settled, 0, nc.gpsimd)
-                scale_tail(settled, 1, nc.gpsimd if early(settled + 1) else nc.vector)
+                if early(settled + 1):
+                    scale_tail(settled, 1, nc.gpsimd)
             if quantises(r):
                 quantise(r)
+            if settled is not None and not early(settled + 1):
+                scale_tail(settled, 1, nc.vector)
             if live(r):
                 exponentials(r, 0)
+            if r == N_PAIRS - 1:
+                statistics(r - 1)
             if live(r):
                 row_max(r, 1)
             if live(r + 1):
@@ -348,7 +362,11 @@ def tile_adaptiveinputsoftmax_pa_t_kernel(
             if live(r + 3):
                 group_h(r + 3, 0)
             if settled is not None:
-                store(settled, 0, PAIR)
+                if early(settled + 1):
+                    store(settled, 0, PAIR)
+                else:
+                    store(settled, 1, 1)
+                    store(settled, 0, 1)
             if live(r + X_AHEAD + 2):
                 transpose_x(r + X_AHEAD + 2)
             if live(r + X_AHEAD):
@@ -361,17 +379,18 @@ def tile_adaptiveinputsoftmax_pa_t_kernel(
                 exponentials(r, 1)
             if live(r + 3):
                 group_h(r + 3, 1)
-            if live(r - 1) and r - 1 < N_PAIRS - 1:
+            if live(r - 1) and early(r - 1):
                 reciprocals(r - 1)
+            elif live(r - 1) and r < N_PAIRS - 1:
+                statistics(r - 1)
             if live(r + 1):
                 row_max(r + 1, 0)
-            if closing is not None:
-                last = closing == N_PAIRS - 1
-                for tiles in ((slice(0, 1), slice(1, 2)) if last else (slice(0, PAIR),)):
-                    if last:
-                        reciprocals(closing, tiles)
-                    cluster_probabilities(closing, tiles)
-                    for jj in range(tiles.start, tiles.stop):
-                        scale_tail(closing, jj, nc.vector)
-                        scale_head(closing, jj, nc.vector)
-                        store(closing, jj, 1)
+            if closing is not None and closing < N_PAIRS - 1:
+                for jj in range(PAIR):
+                    finish(closing, jj)
+                    if r == N_PAIRS - 1 and jj == 0:
+                        statistics(r, slice(0, 1))
+            elif closing is not None:
+                statistics(closing, slice(1, 2))
+                for jj in range(PAIR):
+                    finish(closing, jj)

@@ -75,6 +75,26 @@ def tile_adaptiveinputsoftmax_pa_t_kernel(
         bank_logits = ctx.enter_context(tc.psum_pool(name="bank_logits", bufs=3))
         ctx.enter_context(tc.manual_schedule())
 
+        def logits_bank():
+            both = bank_logits.tile([P, 2, HEAD], F32)
+            return both
+
+        zeros = const.tile([P, 2 * HEAD], BF16)
+        nc.gpsimd.memset(zeros[:].bitcast(I32), 0)
+        warm_bank = logits_bank()
+
+        def warm_up(times):
+            for n in range(times):
+                nc.tensor.matmul(
+                    out=warm_bank[:].rearrange("p k n -> p (k n)"),
+                    lhsT=zeros[:, 0:P],
+                    rhs=zeros[:],
+                    start=True,
+                    stop=True,
+                )
+
+        warm_up(4)
+
         w_scales = const.tile([P, ALL_COLS], U8, align_bytes=64)
         for first, end in ((PROJ_AT, PROJ_AT + PROJ), (HEAD_AT, ALL_COLS)):
             nc.vector.memset(w_scales[:, first:end].bitcast(I32), 0)
@@ -223,7 +243,7 @@ def tile_adaptiveinputsoftmax_pa_t_kernel(
 
         def logits(i):
             for jj in range(PAIR):
-                both = bank_logits.tile([P, 2, HEAD], F32)
+                both = logits_bank()
                 for half, (tokens, at) in enumerate(
                     ((tokens_of_x(i, jj), HEAD_AT), (tokens_of_h(i, jj), TAIL_AT))
                 ):
@@ -327,6 +347,7 @@ def tile_adaptiveinputsoftmax_pa_t_kernel(
             if quantises(r):
                 open_round(r)
         transpose_x(0)
+        warm_up(2)
 
         def early(i):
             return 0 <= i < N_PAIRS - CLOSING_PAIRS
@@ -362,8 +383,11 @@ def tile_adaptiveinputsoftmax_pa_t_kernel(
             if live(r + 3):
                 group_h(r + 3, 0)
             if settled is not None:
-                if early(settled + 1):
+                if early(settled + 2):
                     store(settled, 0, PAIR)
+                elif early(settled + 1):
+                    store(settled, 0, 1)
+                    store(settled, 1, 1)
                 else:
                     store(settled, 1, 1)
                     store(settled, 0, 1)

@@ -347,7 +347,7 @@ def tile_adaptiveinputsoftmax_pa_t_kernel(
             if quantises(r):
                 open_round(r)
         transpose_x(0)
-        warm_up(2)
+        warm_up(4)
 
         def early(i):
             return 0 <= i < N_PAIRS - CLOSING_PAIRS

@@ -27,7 +27,7 @@ N_PAIRS = PER_PARTITION // PAIR
 BLOCK = 4
 N_BLOCKS = PER_PARTITION // BLOCK
 assert (4 * BLOCK * PROBS) % 32 == 0
-SCALAR_TAKES_X = (10, 20)
+SCALAR_TAKES_X = (15,)
 CLOSING_PAIRS = 3
 PAIR_WORDS = PAIR * P
 

@@ -55,9 +55,7 @@ def tile_adaptiveinputsoftmax_pa_t_kernel(
     out_1,
 ):
     nc = tc.nc
-    x_pairs = x.flatten_outer_dims().rearrange(
-        "(p i j) d -> i p (j d)", p=P, i=N_PAIRS, j=PAIR
-    )
+    x_rows = x.flatten_outer_dims().rearrange("(p c) d -> p (c d)", p=P)
     probs_blocks = out_0.flatten_outer_dims().rearrange(
         "(p s j) d -> s p (j d)", p=P, s=N_BLOCKS, j=BLOCK
     )
@@ -65,7 +63,6 @@ def tile_adaptiveinputsoftmax_pa_t_kernel(
 
     with ExitStack() as ctx:
         const = ctx.enter_context(tc.tile_pool(name="const", bufs=1))
-        x_pool = ctx.enter_context(tc.tile_pool(name="x_pool", bufs=N_PAIRS))
         grouped = ctx.enter_context(tc.tile_pool(name="grouped", bufs=5))
         packed = ctx.enter_context(tc.tile_pool(name="packed", bufs=X_AHEAD + 3))
         soft = ctx.enter_context(tc.tile_pool(name="soft", bufs=7))
@@ -112,16 +109,13 @@ def tile_adaptiveinputsoftmax_pa_t_kernel(
 
         clusters = const.tile([P, 2, PER_PARTITION], F32)
 
-        x_sb = {}
+        x_sb = const.tile([P, PER_PARTITION, FEATURES], BF16)
 
-        def load_x(i):
-            x_pair = x_pool.tile([P, PAIR, FEATURES], BF16)
-            flat = x_pair[:].rearrange("p j d -> p (j d)")
-            width = FEATURES if i == 0 else PAIR * FEATURES
-            for first in range(0, PAIR * FEATURES, width):
-                cols = slice(first, first + width)
-                nc.sync.dma_start(out=flat[:, cols], in_=x_pairs[i][:, cols])
-            x_sb[i] = x_pair
+        def load_x(first, tiles):
+            nc.sync.dma_start(
+                out=x_sb[:, first : first + tiles, :].rearrange("p c d -> p (c d)"),
+                in_=x_rows[:, first * FEATURES : (first + tiles) * FEATURES],
+            )
 
         def load_weight(words, scales, at, cols):
             for quadrant in range(4):
@@ -134,16 +128,16 @@ def tile_adaptiveinputsoftmax_pa_t_kernel(
                 in_=words[0].rearrange("p n t -> p (n t)").bitcast(I32),
             )
 
-        load_x(0)
+        load_x(0, PAIR)
         load_weight(tail_proj_0_words, tail_proj_0_scales, PROJ_AT, PROJ)
-        for i in range(1, 5):
-            load_x(i)
+        load_x(2, PAIR)
+        load_x(4, PAIR)
+        load_x(6, 2 * PAIR)
         load_weight(head_weight_words, head_weight_scales, HEAD_AT, HEAD)
-        for i in range(5, 5):
-            load_x(i)
         load_weight(tail_w_0_words, tail_w_0_scales, TAIL_AT, TAIL)
-        for i in range(5, N_PAIRS):
-            load_x(i)
+        load_x(10, PAIR)
+        for first in range(12, PER_PARTITION, 2 * PAIR):
+            load_x(first, 2 * PAIR)
 
         def reorder_proj():
             nc.vector.tensor_copy(
@@ -177,7 +171,7 @@ def tile_adaptiveinputsoftmax_pa_t_kernel(
             for jj in range(PAIR):
                 if jj == 0 or i == 0:
                     xt = bank_xt.tile([P, PAIR, 2, P], F32)
-                words = x_sb[i][:, jj, :].bitcast(F32)
+                words = x_sb[:, PAIR * i + jj, :].bitcast(F32)
                 for u in range(2):
                     nc.tensor.transpose(
                         out=xt[:, jj, u, :],

from contextlib import ExitStack

import concourse.mybir as mybir
from concourse.masks import make_identity

F32 = mybir.dt.float32
BF16 = mybir.dt.bfloat16
I32 = mybir.dt.int32
U32 = mybir.dt.uint32
U8 = mybir.dt.uint8
FP8X4 = mybir.dt.float8_e4m3fn_x4
ALU = mybir.AluOpType
ACT = mybir.ActivationFunctionType

P = 128
PACK = 4
TOKENS = 8 * 1024
FEATURES = 512
HEAD = 256
HEAD_TOKENS = 254
PROJ = 512
TAIL = 256
PROBS = HEAD_TOKENS + TAIL
PER_PARTITION = TOKENS // P
PAIR = 2
N_PAIRS = PER_PARTITION // PAIR
BLOCK = 4
N_BLOCKS = PER_PARTITION // BLOCK
assert (4 * BLOCK * PROBS) % 32 == 0
SCALAR_TAKES_X = (15,)
CLOSING_PAIRS = 3
PAIR_WORDS = PAIR * P

X_AHEAD = 4
H_AHEAD = 1

PROJ_AT = 0
HEAD_AT = PROJ
TAIL_AT = PROJ + HEAD
ALL_COLS = PROJ + HEAD + TAIL

FLOPS = 2 * TOKENS * FEATURES * ALL_COLS


def tile_adaptiveinputsoftmax_pa_t_kernel(
    tc,
    x,
    head_weight_words,
    head_weight_scales,
    tail_proj_0_words,
    tail_proj_0_scales,
    tail_w_0_words,
    tail_w_0_scales,
    out_0,
    out_1,
):
    nc = tc.nc
    x_rows = x.flatten_outer_dims().rearrange("(p c) d -> p (c d)", p=P)
    probs_blocks = out_0.flatten_outer_dims().rearrange(
        "(p s j) d -> s p (j d)", p=P, s=N_BLOCKS, j=BLOCK
    )
    other_cluster = out_1.rearrange("n t o -> (n t o)").rearrange("(p c) -> p c", p=P)

    with ExitStack() as ctx:
        const = ctx.enter_context(tc.tile_pool(name="const", bufs=1))
        grouped = ctx.enter_context(tc.tile_pool(name="grouped", bufs=5))
        packed = ctx.enter_context(tc.tile_pool(name="packed", bufs=X_AHEAD + 3))
        soft = ctx.enter_context(tc.tile_pool(name="soft", bufs=7))
        result = ctx.enter_context(tc.tile_pool(name="result", bufs=3))
        bank_xt = ctx.enter_context(tc.psum_pool(name="bank_xt", bufs=2))
        bank_ht = ctx.enter_context(tc.psum_pool(name="bank_ht", bufs=3))
        bank_logits = ctx.enter_context(tc.psum_pool(name="bank_logits", bufs=3))
        ctx.enter_context(tc.manual_schedule())

        def logits_bank():
            both = bank_logits.tile([P, 2, HEAD], F32)
            return both

        zeros = const.tile([P, 2 * HEAD], BF16)
        nc.gpsimd.memset(zeros[:].bitcast(I32), 0)
        warm_bank = logits_bank()

        def warm_up(times):
            for n in range(times):
                nc.tensor.matmul(
                    out=warm_bank[:].rearrange("p k n -> p (k n)"),
                    lhsT=zeros[:, 0:P],
                    rhs=zeros[:],
                    start=True,
                    stop=True,
                )

        warm_up(4)

        w_scales = const.tile([P, ALL_COLS], U8, align_bytes=64)
        for first, end in ((PROJ_AT, PROJ_AT + PROJ), (HEAD_AT, ALL_COLS)):
            nc.vector.memset(w_scales[:, first:end].bitcast(I32), 0)
        w_words = const.tile([P, ALL_COLS], U32, align_bytes=64)
        proj_scales = const.tile([P, PROJ], U8, align_bytes=64)
        proj_words = const.tile([P, PROJ], U32, align_bytes=64)

        warm_in = const.tile([P, 1], F32)
        warm_out = const.tile([P, 1], F32)
        nc.vector.memset(warm_in[:], 0.0)
        nc.scalar.activation(out=warm_out[:], in_=warm_in[:], func=ACT.Exp)

        ident_f32 = const.tile([P, P], F32)
        make_identity(nc, ident_f32[:])

        clusters = const.tile([P, 2, PER_PARTITION], F32)

        x_sb = const.tile([P, PER_PARTITION, FEATURES], BF16)

        def load_x(first, tiles):
            nc.sync.dma_start(
                out=x_sb[:, first : first + tiles, :].rearrange("p c d -> p (c d)"),
                in_=x_rows[:, first * FEATURES : (first + tiles) * FEATURES],
            )

        def load_weight(words, scales, at, cols):
            for quadrant in range(4):
                nc.sync.dma_start(
                    out=w_scales[32 * quadrant : 32 * quadrant + 4, at : at + cols].bitcast(I32),
                    in_=scales[0, 4 * quadrant : 4 * quadrant + 4, :].bitcast(I32),
                )
            nc.sync.dma_start(
                out=w_words[:, at : at + cols].bitcast(I32),
                in_=words[0].rearrange("p n t -> p (n t)").bitcast(I32),
            )

        load_x(0, PAIR)
        load_weight(tail_proj_0_words, tail_proj_0_scales, PROJ_AT, PROJ)
        load_x(2, PAIR)
        load_x(4, PAIR)
        load_x(6, 2 * PAIR)
        load_weight(head_weight_words, head_weight_scales, HEAD_AT, HEAD)
        load_weight(tail_w_0_words, tail_w_0_scales, TAIL_AT, TAIL)
        load_x(10, PAIR)
        for first in range(12, PER_PARTITION, 2 * PAIR):
            load_x(first, 2 * PAIR)

        def reorder_proj():
            nc.vector.tensor_copy(
                out=proj_words[:].bitcast(I32).rearrange("p (t m) -> p t m", t=PACK),
                in_=w_words[:, PROJ_AT : PROJ_AT + PROJ].bitcast(I32).rearrange("p (m t) -> p t m", t=PACK),
            )
            nc.vector.tensor_copy(
                out=proj_scales[:].rearrange("p (t m) -> p m t", t=PACK),
                in_=w_scales[:, PROJ_AT : PROJ_AT + PROJ].rearrange("p (m t) -> p m t", t=PACK),
            )

        xt_bank, ht_bank, logit_bank = {}, {}, {}
        to_quantise, codes, scales = {}, {}, {}
        neg_max, exps, sums, probs, inv_sum = {}, {}, {}, {}, {}

        def live(i):
            return 0 <= i < N_PAIRS

        def open_round(r):
            values = grouped.tile([P, 2 * PAIR_WORDS * PACK], BF16, align_bytes=64)
            to_quantise[r] = values

        def values_of_x(i):
            return to_quantise[i - X_AHEAD][:, 0 : PAIR_WORDS * PACK]

        def values_of_h(i, jj):
            first = (PAIR_WORDS + jj * P) * PACK
            return to_quantise[i - H_AHEAD][:, first : first + P * PACK]

        def transpose_x(i):
            for jj in range(PAIR):
                if jj == 0 or i == 0:
                    xt = bank_xt.tile([P, PAIR, 2, P], F32)
                words = x_sb[:, PAIR * i + jj, :].bitcast(F32)
                for u in range(2):
                    nc.tensor.transpose(
                        out=xt[:, jj, u, :],
                        in_=words[:, u : FEATURES // 2 : 2],
                        identity=ident_f32[:],
                    )
                xt_bank[i, jj] = xt

        def group_x(i):
            words = values_of_x(i).bitcast(F32).rearrange("p (j r u) -> p j r u", j=PAIR, u=2)
            if i == 0:
                for jj, copy in enumerate((nc.vector.tensor_copy, nc.scalar.copy)):
                    copy(
                        out=words[:, jj, :, :],
                        in_=xt_bank[i, jj][:, jj, :, :].rearrange("p u r -> p r u"),
                    )
            else:
                copy = nc.scalar.copy if i in SCALAR_TAKES_X else nc.vector.tensor_copy
                copy(out=words, in_=xt_bank[i, 0][:].rearrange("p j u r -> p j r u"))

        def quantise(r):
            round_codes = packed.tile([P, 2 * PAIR_WORDS], U32, align_bytes=64)
            round_scales = packed.tile([P, 2 * PAIR_WORDS], U8, align_bytes=64)
            first = 0 if live(r + X_AHEAD) else PAIR_WORDS
            end = 2 * PAIR_WORDS if live(r + H_AHEAD) else PAIR_WORDS
            nc.vector.quantize_mx(
                out=round_codes[:, first:end].bitcast(FP8X4),
                scales=round_scales[:, first:end],
                in_=to_quantise[r][:, first * PACK : end * PACK],
            )
            codes[r] = round_codes
            scales[r] = round_scales

        def tokens_of_x(i, jj):
            r, first = i - X_AHEAD, jj * P
            return codes[r][:, first : first + P].bitcast(FP8X4), scales[r][:, first : first + P]

        def tokens_of_h(i, jj):
            r, first = i - H_AHEAD, PAIR_WORDS + jj * P
            return codes[r][:, first : first + P].bitcast(FP8X4), scales[r][:, first : first + P]

        def project(i):
            for jj in range(PAIR):
                ht = bank_ht.tile([P, PACK, P], F32)
                x_codes, x_scales = tokens_of_x(i, jj)
                for t in range(PACK):
                    nc.tensor.matmul_mx(
                        out=ht[:, t, :],
                        lhsT=proj_words[:, t * P : (t + 1) * P].bitcast(FP8X4),
                        lhsT_scale=proj_scales[:, t * P : (t + 1) * P],
                        rhs=x_codes,
                        rhs_scale=x_scales,
                        start=True,
                        stop=True,
                    )
                ht_bank[i, jj] = ht

        def group_h(i, jj):
            nc.scalar.copy(
                out=values_of_h(i, jj).rearrange("p (r t) -> p r t", t=PACK),
                in_=ht_bank[i, jj][:].rearrange("p t r -> p r t"),
            )

        def logits(i):
            for jj in range(PAIR):
                both = logits_bank()
                for half, (tokens, at) in enumerate(
                    ((tokens_of_x(i, jj), HEAD_AT), (tokens_of_h(i, jj), TAIL_AT))
                ):
                    nc.tensor.matmul_mx(
                        out=both[:, half, :],
                        lhsT=tokens[0],
                        lhsT_scale=tokens[1],
                        rhs=w_words[:, at : at + HEAD].bitcast(FP8X4),
                        rhs_scale=w_scales[:, at : at + HEAD],
                        start=True,
                        stop=True,
                    )
                logit_bank[i, jj] = both

        def row_max(i, jj):
            if jj == 0:
                minus_max = soft.tile([P, PAIR, 2], F32)
                neg_max[i] = minus_max
            nc.vector.tensor_reduce(
                out=neg_max[i][:, jj, :],
                in_=logit_bank[i, jj][:],
                axis=mybir.AxisListType.X,
                op=ALU.max,
                negate=True,
            )

        def exponentials(i, jj):
            if jj == 0:
                e = soft.tile([P, PAIR, 2, HEAD], F32)
                e_sum = soft.tile([P, PAIR, 2], F32)
                exps[i] = e
                sums[i] = e_sum
            for half in range(2):
                nc.scalar.activation(
                    out=exps[i][:, jj, half, :],
                    in_=logit_bank[i, jj][:, half, :],
                    func=ACT.Exp,
                    bias=neg_max[i][:, jj, half : half + 1],
                    accum_out=sums[i][:, jj, half : half + 1],
                )

        def reciprocals(i, tiles=slice(0, PAIR)):
            if tiles.start == 0:
                inv = soft.tile([P, PAIR, 2], F32)
                inv_sum[i] = inv
            nc.vector.reciprocal(out=inv_sum[i][:, tiles, :], in_=sums[i][:, tiles, :])

        def open_probs(i):
            if i % 2 == 0:
                probs_block = result.tile([P, BLOCK, PROBS], F32)
                probs[i // 2] = probs_block

        def cluster_probabilities(i, tiles=slice(0, PAIR)):
            nc.vector.tensor_tensor(
                out=clusters[:, :, PAIR * i + tiles.start : PAIR * i + tiles.stop],
                in0=exps[i][:, tiles, 0, HEAD_TOKENS:HEAD].rearrange("p j k -> p k j"),
                in1=inv_sum[i][:, tiles, 0].unsqueeze(1).to_broadcast([P, 2, tiles.stop - tiles.start]),
                op=ALU.mult,
            )
            if i == N_PAIRS - 1 and tiles.stop == PAIR:
                nc.sync.dma_start(out=other_cluster, in_=clusters[:, 1, :])

        def scale_head(i, jj, engine):
            out = probs[i // 2][:, PAIR * (i % 2) + jj, 0:HEAD_TOKENS]
            e_head = exps[i][:, jj, 0, 0:HEAD_TOKENS]
            factor = inv_sum[i][:, jj, 0:1]
            engine.tensor_scalar(
                out=out, in0=e_head, scalar1=factor, scalar2=0.0, op0=ALU.mult, op1=ALU.add
            )

        def scale_tail(i, jj, engine):
            engine.tensor_scalar(
                out=probs[i // 2][:, PAIR * (i % 2) + jj, HEAD_TOKENS:PROBS],
                in0=exps[i][:, jj, 1, :],
                scalar1=inv_sum[i][:, jj, 1:2],
                scalar2=clusters[:, 0, PAIR * i + jj : PAIR * i + jj + 1],
                op0=ALU.mult,
                op1=ALU.mult,
            )

        def store(i, first_tile, tiles):
            j = PAIR * (i % 2) + first_tile
            written = slice(j * PROBS // 8 * 8, (j + tiles) * PROBS // 8 * 8)
            flat_rows = probs[i // 2][:].rearrange("p j d -> p (j d)")
            nc.sync.dma_start(out=probs_blocks[i // 2][:, written], in_=flat_rows[:, written])

        def statistics(i, tiles=slice(0, PAIR)):
            reciprocals(i, tiles)
            cluster_probabilities(i, tiles)

        def finish(i, jj):
            scale_head(i, jj, nc.vector)
            scale_tail(i, jj, nc.vector)
            store(i, jj, 1)

        def quantises(r):
            return live(r + X_AHEAD) or live(r + H_AHEAD)

        FIRST_ROUND = -X_AHEAD - 1
        for r in (FIRST_ROUND, FIRST_ROUND + 1):
            if quantises(r):
                open_round(r)
        transpose_x(0)
        warm_up(4)

        def early(i):
            return 0 <= i < N_PAIRS - CLOSING_PAIRS

        for r in range(FIRST_ROUND, N_PAIRS + 1):
            settled = r - 2 if early(r - 2) else None
            closing = r - 1 if N_PAIRS - CLOSING_PAIRS <= r - 1 < N_PAIRS else None
            if quantises(r + 2):
                open_round(r + 2)
            if live(r):
                open_probs(r)
            if r + X_AHEAD + 1 in SCALAR_TAKES_X:
                group_x(r + X_AHEAD + 1)
            if settled is not None:
                scale_head(settled, 1, nc.vector)
                cluster_probabilities(settled)
                scale_tail(settled, 0, nc.gpsimd)
                scale_head(settled, 0, nc.gpsimd)
                if early(settled + 1):
                    scale_tail(settled, 1, nc.gpsimd)
            if quantises(r):
                quantise(r)
            if settled is not None and not early(settled + 1):
                scale_tail(settled, 1, nc.vector)
            if live(r):
                exponentials(r, 0)
            if r == N_PAIRS - 1:
                statistics(r - 1)
            if live(r):
                row_max(r, 1)
            if live(r + 1):
                logits(r + 1)
            if live(r + 3):
                group_h(r + 3, 0)
            if settled is not None:
                if early(settled + 2):
                    store(settled, 0, PAIR)
                elif early(settled + 1):
                    store(settled, 0, 1)
                    store(settled, 1, 1)
                else:
                    store(settled, 1, 1)
                    store(settled, 0, 1)
            if live(r + X_AHEAD + 2):
                transpose_x(r + X_AHEAD + 2)
            if live(r + X_AHEAD):
                project(r + X_AHEAD)
            if live(r + X_AHEAD + 1) and r + X_AHEAD + 1 not in SCALAR_TAKES_X:
                group_x(r + X_AHEAD + 1)
            if r == FIRST_ROUND:
                reorder_proj()
            if live(r):
                exponentials(r, 1)
            if live(r + 3):
                group_h(r + 3, 1)
            if live(r - 1) and early(r - 1):
                reciprocals(r - 1)
            elif live(r - 1) and r < N_PAIRS - 1:
                statistics(r - 1)
            if live(r + 1):
                row_max(r + 1, 0)
            if closing is not None and closing < N_PAIRS - 1:
                for jj in range(PAIR):
                    finish(closing, jj)
                    if r == N_PAIRS - 1 and jj == 0:
                        statistics(r, slice(0, 1))
            elif closing is not None:
                statistics(closing, slice(1, 2))
                for jj in range(PAIR):
                    finish(closing, jj)
